import numpy as np
import ml_dtypes


def mxq(x, axis, fmt="e4m3"):
    dtype, down = {"e4m3": (ml_dtypes.float8_e4m3fn, 7), "e5m2": (ml_dtypes.float8_e5m2, 14)}[fmt]
    v = np.moveaxis(np.asarray(x, np.float32).astype(ml_dtypes.bfloat16).astype(np.float64), axis, -1)
    blocks = v.reshape(v.shape[:-1] + (-1, 32))
    amax = np.abs(blocks).max(-1, keepdims=True)
    byte = np.maximum(np.where(amax > 0, np.frexp(amax)[1] - 1 + 127, 0) - down, 1)
    scale = np.exp2(byte - 127.0)
    codes = (blocks / scale).astype(np.float32).astype(dtype).astype(np.float64)
    return np.moveaxis((codes * scale).reshape(v.shape), -1, axis)


WIDE = False


def mx_kscale(k):
    if not WIDE:
        return np.ones(k)
    levels = np.array([10, -10, 5, -5, 0])
    a = np.random.permutation(np.resize(levels, k // 512 * 4)).reshape(k // 512, 4)
    idx = np.arange(k)
    return np.exp2(a[idx // 512, idx % 128 // 32])


BF16 = ml_dtypes.bfloat16


def bf(x):
    return np.asarray(x, np.float32).astype(BF16)


def f64(x):
    return np.asarray(x).astype(np.float64)


NB, T, N, H, HD, CO = 1, 2, 512, 8, 128, 1024
B = NB * T
C = H * HD
VS = 10.0 * H / N


def setup_inputs():
    t = mx_kscale(C)
    sg = np.sign(np.random.standard_normal(C))
    return {"q": bf(np.random.standard_normal((B, H, N, HD)) * 1.5),
            "k": bf(np.random.standard_normal((B, H, N, HD)) * 1.5),
            "v": bf(np.abs(np.random.standard_normal((B, H, N, HD))) * VS * (sg * t).reshape(H, HD)[None, :, None, :]),
            "w_proj": bf(np.random.standard_normal((CO, C)) * 0.5 / np.sqrt(C) / t[None, :])}


def reference(q, k, v, w_proj):
    s = f64(q) @ f64(k).transpose(0, 1, 3, 2) * HD ** -0.5
    e = np.exp(s - s.max(1, keepdims=True))
    attn = e / e.sum(1, keepdims=True)
    o = mxq(attn, 3, "e4m3") @ mxq(f64(v), 2, "e4m3")
    o = o.transpose(0, 2, 1, 3).reshape(B, N, C)
    wq = mxq(f64(w_proj), 1, "e4m3")
    return mxq(o, 2, "e4m3") @ wq.T

@@ -1,0 +1,308 @@
+from contextlib import ExitStack
+
+import concourse.mybir as mybir
+from concourse.masks import make_identity
+
+F32 = mybir.dt.float32
+BF16 = mybir.dt.bfloat16
+U32 = mybir.dt.uint32
+U8 = mybir.dt.uint8
+FP8X4 = mybir.dt.float8_e4m3fn_x4
+ALU = mybir.AluOpType
+ACT = mybir.ActivationFunctionType
+
+P = 128
+PACK = 4
+FRAMES = 2
+HEADS = 8
+TOKENS = 512
+HEAD_DIM = 128
+CHANNELS = HEADS * HEAD_DIM
+C_OUT = 1024
+PASSES = CHANNELS // (P * PACK)
+BANK = 512
+
+CHUNK = 64
+UNIT_COLS = CHUNK * PACK
+UNITS_PER_FRAME = TOKENS // CHUNK
+UNITS = FRAMES * UNITS_PER_FRAME
+HEADS_PER_BANK = BANK // UNIT_COLS
+SCORE_BANKS = HEADS // HEADS_PER_BANK
+TILE_Q = 128
+TILE_COLS = TILE_Q * PACK
+
+FLOPS = 2 * FRAMES * HEADS * TOKENS * TOKENS * HEAD_DIM * 2 + 2 * FRAMES * TOKENS * CHANNELS * C_OUT
+
+
+def tile_attention2_pa_kernel(tc, q, k, v, w_proj, out):
+    nc = tc.nc
+    with ExitStack() as stack:
+        const = stack.enter_context(tc.tile_pool(name="const", bufs=1))
+        raw = stack.enter_context(tc.tile_pool(name="raw", bufs=1))
+        keep = stack.enter_context(tc.tile_pool(name="keep", bufs=1))
+        single = stack.enter_context(tc.tile_pool(name="single", bufs=1))
+        double = stack.enter_context(tc.tile_pool(name="double", bufs=2))
+        triple = stack.enter_context(tc.tile_pool(name="triple", bufs=3))
+        score_psum = stack.enter_context(tc.psum_pool(name="score_psum", bufs=1))
+        aux_psum = stack.enter_context(tc.psum_pool(name="aux_psum", bufs=4))
+
+        identity = const.tile([P, P], BF16)
+        make_identity(nc, identity[:])
+
+        def load_kq(b):
+            kq_raw = raw.tile([P, HEADS, 2 * PACK, HEAD_DIM], BF16, name="kq_raw")
+            half = HEADS // 2
+            for h0 in (0, half):
+                for x0, src in ((0, k), (PACK, q)):
+                    nc.sync.dma_start(
+                        out=kq_raw[:, h0 : h0 + half, x0 : x0 + PACK, :].rearrange("p h x d -> p h (x d)"),
+                        in_=src[b, h0 : h0 + half].rearrange("h (p x) d -> p h (x d)", x=PACK),
+                    )
+            return kq_raw
+
+        def load_v(b):
+            v_raw = raw.tile([P, HEADS, PACK, HEAD_DIM], BF16, name="v_raw%d" % b)
+            nc.sync.dma_start(
+                out=v_raw[:].rearrange("p h t d -> p h (t d)"),
+                in_=v[b].rearrange("h (p t) d -> p h (t d)", t=PACK),
+            )
+            return v_raw
+
+        kq_raw = {0: load_kq(0)}
+        w_raw = raw.tile([P, C_OUT // P, CHANNELS], BF16)
+        w_rows = w_proj.rearrange("(i p) c -> p i c", p=P)
+        for i0 in (0, 4):
+            nc.sync.dma_start(out=w_raw[:, i0 : i0 + 4, :], in_=w_rows[:, i0 : i0 + 4, :])
+        v_raw = {0: load_v(0)}
+
+        kqT = {}
+        v_grouped = {}
+        v_codes = {}
+        v_scales = {}
+        for b in range(FRAMES):
+            kqT[b] = keep.tile([P, HEADS, 2 * PACK, P], BF16, name="kqT%d" % b)
+            v_codes[b] = keep.tile([P, HEADS * HEAD_DIM], U32, name="v_codes%d" % b, align_bytes=64)
+            v_scales[b] = keep.tile([P, HEADS * HEAD_DIM], U8, name="v_scales%d" % b, align_bytes=64)
+        w_grouped = keep.tile([P, PASSES, C_OUT, PACK], BF16, align_bytes=64)
+        w_codes = keep.tile([P, PASSES * C_OUT], U32, align_bytes=64)
+        w_scales = keep.tile([P, PASSES * C_OUT], U8, align_bytes=64)
+
+        def transpose_kq_head(b, h, copy_out):
+            kq_ps = aux_psum.tile([P, 2 * PACK, P], BF16, tag="aux")
+            for x in range(2 * PACK):
+                nc.tensor.transpose(kq_ps[:, x, :], kq_raw[b][:, h, x, :], identity[:])
+            copy_out(out=kqT[b][:, h, :, :], in_=kq_ps[:])
+
+        def group_v_head(b, h):
+            nc.scalar.copy(out=v_grouped[b][:, h, :, :], in_=v_raw[b][:, h, :, :].rearrange("p t d -> p d t"))
+
+        def quantise_v(b):
+            nc.vector.quantize_mx(
+                out=v_codes[b][:].bitcast(FP8X4),
+                scales=v_scales[b][:],
+                in_=v_grouped[b][:].rearrange("p h d t -> p (h d t)"),
+            )
+
+        def transpose_w_rows(i):
+            w_ps = aux_psum.tile([P, PASSES * PACK, P], BF16, tag="aux")
+            for c in range(PASSES * PACK):
+                nc.tensor.transpose(w_ps[:, c, :], w_raw[:, i, c * P : (c + 1) * P], identity[:])
+            nc.scalar.copy(
+                out=w_grouped[:, :, i * P : (i + 1) * P, :],
+                in_=w_ps[:].rearrange("p (g t) r -> p g r t", t=PACK),
+            )
+
+        def quantise_w():
+            for g in range(PASSES):
+                nc.vector.quantize_mx(
+                    out=w_codes[:, g * C_OUT : (g + 1) * C_OUT].bitcast(FP8X4),
+                    scales=w_scales[:, g * C_OUT : (g + 1) * C_OUT],
+                    in_=w_grouped[:, g, :, :].rearrange("p r t -> p (r t)"),
+                )
+
+        scores = {}
+        running = {}
+        shifted = {}
+        expd = {}
+        totals = {}
+        recips = {}
+        attn = {}
+
+        def frame_of(u):
+            return u // UNITS_PER_FRAME
+
+        def score_matmuls(u):
+            b = frame_of(u)
+            first = (u % UNITS_PER_FRAME) * CHUNK
+            j, col = first // P, first % P
+            scores[u] = []
+            for bank in range(SCORE_BANKS):
+                s_ps = score_psum.tile([P, HEADS_PER_BANK, CHUNK, PACK], F32, name="s_ps%d" % bank)
+                for i in range(HEADS_PER_BANK):
+                    h = bank * HEADS_PER_BANK + i
+                    for t in range(PACK):
+                        nc.tensor.matmul(
+                            out=s_ps[:, i, :, t],
+                            lhsT=kqT[b][:, h, t, :],
+                            rhs=kqT[b][:, h, PACK + j, col : col + CHUNK],
+                            start=True,
+                            stop=True,
+                        )
+                scores[u].append(s_ps)
+
+        def bank_view(s_ps):
+            return s_ps[:].rearrange("p i n t -> p i (n t)")
+
+        def seed_maximum(u):
+            run_a = double.tile([P, HEADS_PER_BANK, UNIT_COLS], F32)
+            run_b = double.tile([P, HEADS_PER_BANK, UNIT_COLS], F32)
+            nc.scalar.copy(out=run_a[:], in_=bank_view(scores[u][0]))
+            nc.scalar.copy(out=run_b[:], in_=bank_view(scores[u][1]))
+            running[u] = (run_a, run_b)
+
+        def shift_by_maximum(u):
+            run_a, run_b = running[u]
+            nc.vector.tensor_tensor(out=run_a[:], in0=bank_view(scores[u][2]), in1=run_a[:], op=ALU.max)
+            nc.vector.tensor_tensor(out=run_b[:], in0=bank_view(scores[u][3]), in1=run_b[:], op=ALU.max)
+            nc.vector.tensor_tensor(out=run_a[:], in0=run_a[:], in1=run_b[:], op=ALU.max)
+            top = double.tile([P, UNIT_COLS], F32)
+            nc.vector.tensor_tensor(out=top[:], in0=run_a[:, 0, :], in1=run_a[:, 1, :], op=ALU.max)
+            diff = single.tile([P, HEADS, UNIT_COLS], F32)
+            for bank, s_ps in enumerate(scores[u]):
+                nc.vector.tensor_tensor(
+                    out=diff[:, bank * HEADS_PER_BANK : (bank + 1) * HEADS_PER_BANK, :],
+                    in0=bank_view(s_ps),
+                    in1=top[:].unsqueeze(1).to_broadcast([P, HEADS_PER_BANK, UNIT_COLS]),
+                    op=ALU.subtract,
+                )
+            shifted[u] = diff
+
+        def exponentials(u):
+            e = triple.tile([P, HEADS, UNIT_COLS], F32)
+            nc.scalar.activation(out=e[:], in_=shifted[u][:], func=ACT.Exp, scale=HEAD_DIM**-0.5)
+            expd[u] = e
+
+        def sum_over_heads(u):
+            e = expd[u]
+            four = single.tile([P, 4, UNIT_COLS], F32)
+            two = single.tile([P, 2, UNIT_COLS], F32)
+            total = double.tile([P, UNIT_COLS], F32)
+            nc.gpsimd.tensor_tensor(out=four[:], in0=e[:, 0:4, :], in1=e[:, 4:8, :], op=ALU.add)
+            nc.gpsimd.tensor_tensor(out=two[:], in0=four[:, 0:2, :], in1=four[:, 2:4, :], op=ALU.add)
+            nc.gpsimd.tensor_tensor(out=total[:], in0=two[:, 0, :], in1=two[:, 1, :], op=ALU.add)
+            totals[u] = total
+
+        def reciprocal_of_sum(u):
+            r = double.tile([P, UNIT_COLS], F32)
+            nc.vector.reciprocal(out=r[:], in_=totals[u][:])
+            recips[u] = r
+
+        def normalise(u):
+            tile_index, half = u // 2, u % 2
+            if half == 0:
+                attn[tile_index] = single.tile([P, HEADS, TILE_COLS], BF16, name="attn", align_bytes=64)
+            nc.vector.tensor_tensor(
+                out=attn[tile_index][:, :, half * UNIT_COLS : (half + 1) * UNIT_COLS],
+                in0=expd[u][:],
+                in1=recips[u][:].unsqueeze(1).to_broadcast([P, HEADS, UNIT_COLS]),
+                op=ALU.mult,
+            )
+
+        o_grouped = {}
+
+        def attention_times_v(m):
+            b = m // (TOKENS // TILE_Q)
+            a_codes = double.tile([P, HEADS * TILE_Q], U32, align_bytes=64)
+            a_scales = double.tile([P, HEADS * TILE_Q], U8, align_bytes=64)
+            nc.vector.quantize_mx(
+                out=a_codes[:].bitcast(FP8X4),
+                scales=a_scales[:],
+                in_=attn[m][:].rearrange("p h c -> p (h c)"),
+            )
+            o_grouped[m] = double.tile([P, PASSES, TILE_Q, PACK], BF16, name="o_grouped", align_bytes=64)
+            for g in range(PASSES):
+                o_ps = aux_psum.tile([P, PACK, TILE_Q], F32, tag="aux")
+                for t in range(PACK):
+                    h = g * PACK + t
+                    cols = slice(h * TILE_Q, (h + 1) * TILE_Q)
+                    nc.tensor.matmul_mx(
+                        out=o_ps[:, t, :],
+                        lhsT=v_codes[b][:, cols].bitcast(FP8X4),
+                        lhsT_scale=v_scales[b][:, cols],
+                        rhs=a_codes[:, cols].bitcast(FP8X4),
+                        rhs_scale=a_scales[:, cols],
+                        start=True,
+                        stop=True,
+                    )
+                nc.scalar.copy(out=o_grouped[m][:, g, :, :], in_=o_ps[:].rearrange("p t n -> p n t"))
+
+        def project(m):
+            b, j = divmod(m, TOKENS // TILE_Q)
+            o_codes = double.tile([P, PASSES * TILE_Q], U32, align_bytes=64)
+            o_scales = double.tile([P, PASSES * TILE_Q], U8, align_bytes=64)
+            nc.vector.quantize_mx(
+                out=o_codes[:].bitcast(FP8X4),
+                scales=o_scales[:],
+                in_=o_grouped[m][:].rearrange("p g n t -> p (g n t)"),
+            )
+            y = double.tile([P, C_OUT], F32)
+            for c0 in range(0, C_OUT, BANK):
+                y_ps = aux_psum.tile([P, BANK], F32, tag="aux")
+                for g in range(PASSES):
+                    o_cols = slice(g * TILE_Q, (g + 1) * TILE_Q)
+                    w_cols = slice(g * C_OUT + c0, g * C_OUT + c0 + BANK)
+                    nc.tensor.matmul_mx(
+                        out=y_ps[:],
+                        lhsT=o_codes[:, o_cols].bitcast(FP8X4),
+                        lhsT_scale=o_scales[:, o_cols],
+                        rhs=w_codes[:, w_cols].bitcast(FP8X4),
+                        rhs_scale=w_scales[:, w_cols],
+                        start=(g == 0),
+                        stop=(g == PASSES - 1),
+                    )
+                nc.scalar.copy(out=y[:, c0 : c0 + BANK], in_=y_ps[:])
+            nc.sync.dma_start(out=out[b].rearrange("(p j) c -> p j c", j=PACK)[:, j, :], in_=y[:])
+
+        for h in range(HEADS):
+            transpose_kq_head(0, h, nc.scalar.copy if h % 2 == 0 else nc.vector.tensor_copy)
+        kq_raw[1] = load_kq(1)
+        v_raw[1] = load_v(1)
+        score_matmuls(0)
+        seed_maximum(0)
+
+        half_frame = UNITS_PER_FRAME // 2
+        for s in range(UNITS + 3):
+            if s % half_frame == 0 and s < UNITS_PER_FRAME:
+                b_next = s // half_frame
+                v_grouped[b_next] = single.tile([P, HEADS, HEAD_DIM, PACK], BF16, name="v_grouped", align_bytes=64)
+            if s < half_frame:
+                for x in (2 * s, 2 * s + 1):
+                    group_v_head(0, x)
+                    transpose_w_rows(x)
+            elif s < UNITS_PER_FRAME:
+                for x in (2 * (s - half_frame), 2 * (s - half_frame) + 1):
+                    transpose_kq_head(1, x, nc.scalar.copy)
+                    group_v_head(1, x)
+
+            if 0 <= s - 2 < UNITS:
+                reciprocal_of_sum(s - 2)
+            if s >= 4 and s % 2 == 0:
+                project((s - 4) // 2)
+            if s < UNITS:
+                shift_by_maximum(s)
+            if s + 1 < UNITS:
+                score_matmuls(s + 1)
+            if s < UNITS:
+                exponentials(s)
+                sum_over_heads(s)
+            if s + 1 < UNITS:
+                seed_maximum(s + 1)
+            if s == half_frame - 1:
+                quantise_v(0)
+                quantise_w()
+            if s == UNITS_PER_FRAME - 1:
+                quantise_v(1)
+            if 0 <= s - 2 < UNITS:
+                normalise(s - 2)
+                if s % 2 == 1:
+                    attention_times_v((s - 3) // 2)

@@ -30,6 +30,7 @@ HEADS_PER_BANK = BANK // UNIT_COLS
 SCORE_BANKS = HEADS // HEADS_PER_BANK
 TILE_Q = 128
 TILE_COLS = TILE_Q * PACK
+TILES_PER_FRAME = TOKENS // TILE_Q
 
 FLOPS = 2 * FRAMES * HEADS * TOKENS * TOKENS * HEAD_DIM * 2 + 2 * FRAMES * TOKENS * CHANNELS * C_OUT
 
@@ -37,6 +38,7 @@ FLOPS = 2 * FRAMES * HEADS * TOKENS * TOKENS * HEAD_DIM * 2 + 2 * FRAMES * TOKEN
 def tile_attention2_pa_kernel(tc, q, k, v, w_proj, out):
     nc = tc.nc
     with ExitStack() as stack:
+        stack.enter_context(tc.manual_schedule())
         const = stack.enter_context(tc.tile_pool(name="const", bufs=1))
         raw = stack.enter_context(tc.tile_pool(name="raw", bufs=1))
         keep = stack.enter_context(tc.tile_pool(name="keep", bufs=1))
@@ -122,6 +124,7 @@ def tile_attention2_pa_kernel(tc, q, k, v, w_proj, out):
 
         scores = {}
         running = {}
+        tops = {}
         shifted = {}
         expd = {}
         totals = {}
@@ -160,19 +163,30 @@ def tile_attention2_pa_kernel(tc, q, k, v, w_proj, out):
             nc.scalar.copy(out=run_b[:], in_=bank_view(scores[u][1]))
             running[u] = (run_a, run_b)
 
+        def maximum_and_reciprocal(u_max, u_rec):
+            half = UNIT_COLS // 2
+            if u_max is not None:
+                run_a, run_b = running[u_max]
+                nc.vector.tensor_tensor(out=run_a[:], in0=bank_view(scores[u_max][2]), in1=run_a[:], op=ALU.max)
+                nc.vector.tensor_tensor(out=run_b[:], in0=bank_view(scores[u_max][3]), in1=run_b[:], op=ALU.max)
+            if u_rec is not None:
+                recips[u_rec] = double.tile([P, UNIT_COLS], F32, name="r")
+                nc.vector.reciprocal(out=recips[u_rec][:, :half], in_=totals[u_rec][:, :half])
+            if u_max is not None:
+                nc.vector.tensor_tensor(out=run_a[:], in0=run_a[:], in1=run_b[:], op=ALU.max)
+            if u_rec is not None:
+                nc.vector.reciprocal(out=recips[u_rec][:, half:], in_=totals[u_rec][:, half:])
+            if u_max is not None:
+                tops[u_max] = double.tile([P, UNIT_COLS], F32, name="top")
+                nc.vector.tensor_tensor(out=tops[u_max][:], in0=run_a[:, 0, :], in1=run_a[:, 1, :], op=ALU.max)
+
         def shift_by_maximum(u):
-            run_a, run_b = running[u]
-            nc.vector.tensor_tensor(out=run_a[:], in0=bank_view(scores[u][2]), in1=run_a[:], op=ALU.max)
-            nc.vector.tensor_tensor(out=run_b[:], in0=bank_view(scores[u][3]), in1=run_b[:], op=ALU.max)
-            nc.vector.tensor_tensor(out=run_a[:], in0=run_a[:], in1=run_b[:], op=ALU.max)
-            top = double.tile([P, UNIT_COLS], F32)
-            nc.vector.tensor_tensor(out=top[:], in0=run_a[:, 0, :], in1=run_a[:, 1, :], op=ALU.max)
             diff = single.tile([P, HEADS, UNIT_COLS], F32)
             for bank, s_ps in enumerate(scores[u]):
                 nc.vector.tensor_tensor(
                     out=diff[:, bank * HEADS_PER_BANK : (bank + 1) * HEADS_PER_BANK, :],
                     in0=bank_view(s_ps),
-                    in1=top[:].unsqueeze(1).to_broadcast([P, HEADS_PER_BANK, UNIT_COLS]),
+                    in1=tops[u][:].unsqueeze(1).to_broadcast([P, HEADS_PER_BANK, UNIT_COLS]),
                     op=ALU.subtract,
                 )
             shifted[u] = diff
@@ -192,26 +206,23 @@ def tile_attention2_pa_kernel(tc, q, k, v, w_proj, out):
             nc.gpsimd.tensor_tensor(out=total[:], in0=two[:, 0, :], in1=two[:, 1, :], op=ALU.add)
             totals[u] = total
 
-        def reciprocal_of_sum(u):
-            r = double.tile([P, UNIT_COLS], F32)
-            nc.vector.reciprocal(out=r[:], in_=totals[u][:])
-            recips[u] = r
-
         def normalise(u):
-            tile_index, half = u // 2, u % 2
+            m, half = u // 2, u % 2
             if half == 0:
-                attn[tile_index] = single.tile([P, HEADS, TILE_COLS], BF16, name="attn", align_bytes=64)
+                attn[m] = single.tile([P, HEADS, TILE_COLS], BF16, name="attn", align_bytes=64)
             nc.vector.tensor_tensor(
-                out=attn[tile_index][:, :, half * UNIT_COLS : (half + 1) * UNIT_COLS],
+                out=attn[m][:, :, half * UNIT_COLS : (half + 1) * UNIT_COLS],
                 in0=expd[u][:],
                 in1=recips[u][:].unsqueeze(1).to_broadcast([P, HEADS, UNIT_COLS]),
                 op=ALU.mult,
             )
 
+        o_banks = {}
         o_grouped = {}
+        y_banks = {}
 
         def attention_times_v(m):
-            b = m // (TOKENS // TILE_Q)
+            b = m // TILES_PER_FRAME
             a_codes = double.tile([P, HEADS * TILE_Q], U32, align_bytes=64)
             a_scales = double.tile([P, HEADS * TILE_Q], U8, align_bytes=64)
             nc.vector.quantize_mx(
@@ -219,7 +230,7 @@ def tile_attention2_pa_kernel(tc, q, k, v, w_proj, out):
                 scales=a_scales[:],
                 in_=attn[m][:].rearrange("p h c -> p (h c)"),
             )
-            o_grouped[m] = double.tile([P, PASSES, TILE_Q, PACK], BF16, name="o_grouped", align_bytes=64)
+            o_banks[m] = []
             for g in range(PASSES):
                 o_ps = aux_psum.tile([P, PACK, TILE_Q], F32, tag="aux")
                 for t in range(PACK):
@@ -234,10 +245,14 @@ def tile_attention2_pa_kernel(tc, q, k, v, w_proj, out):
                         start=True,
                         stop=True,
                     )
+                o_banks[m].append(o_ps)
+
+        def round_o(m):
+            o_grouped[m] = double.tile([P, PASSES, TILE_Q, PACK], BF16, name="o_grouped", align_bytes=64)
+            for g, o_ps in enumerate(o_banks[m]):
                 nc.scalar.copy(out=o_grouped[m][:, g, :, :], in_=o_ps[:].rearrange("p t n -> p n t"))
 
         def project(m):
-            b, j = divmod(m, TOKENS // TILE_Q)
             o_codes = double.tile([P, PASSES * TILE_Q], U32, align_bytes=64)
             o_scales = double.tile([P, PASSES * TILE_Q], U8, align_bytes=64)
             nc.vector.quantize_mx(
@@ -245,7 +260,7 @@ def tile_attention2_pa_kernel(tc, q, k, v, w_proj, out):
                 scales=o_scales[:],
                 in_=o_grouped[m][:].rearrange("p g n t -> p (g n t)"),
             )
-            y = double.tile([P, C_OUT], F32)
+            y_banks[m] = []
             for c0 in range(0, C_OUT, BANK):
                 y_ps = aux_psum.tile([P, BANK], F32, tag="aux")
                 for g in range(PASSES):
@@ -260,8 +275,20 @@ def tile_attention2_pa_kernel(tc, q, k, v, w_proj, out):
                         start=(g == 0),
                         stop=(g == PASSES - 1),
                     )
-                nc.scalar.copy(out=y[:, c0 : c0 + BANK], in_=y_ps[:])
+                y_banks[m].append(y_ps)
+
+        def store(m):
+            b, j = divmod(m, TILES_PER_FRAME)
+            y = double.tile([P, C_OUT], F32)
+            for i, y_ps in enumerate(y_banks[m]):
+                nc.scalar.copy(out=y[:, i * BANK : (i + 1) * BANK], in_=y_ps[:])
             nc.sync.dma_start(out=out[b].rearrange("(p j) c -> p j c", j=PACK)[:, j, :], in_=y[:])
+
+        def unit_or_none(u):
+            return u if 0 <= u < UNITS else None
+
+        def tile_finished_by(u):
+            return u // 2 if 0 <= u < UNITS and u % 2 == 1 else None
 
         for h in range(HEADS):
             transpose_kq_head(0, h, nc.scalar.copy if h % 2 == 0 else nc.vector.tensor_copy)
@@ -271,7 +298,20 @@ def tile_attention2_pa_kernel(tc, q, k, v, w_proj, out):
         seed_maximum(0)
 
         half_frame = UNITS_PER_FRAME // 2
-        for s in range(UNITS + 3):
+        for s in range(UNITS + 6):
+            if unit_or_none(s - 3) is not None:
+                normalise(s - 3)
+
+            if s == half_frame:
+                quantise_v(0)
+                quantise_w()
+            if s == UNITS_PER_FRAME:
+                quantise_v(1)
+
+            if tile_finished_by(s - 4) is not None:
+                round_o(tile_finished_by(s - 4))
+            if tile_finished_by(s - 5) is not None:
+                store(tile_finished_by(s - 5))
             if s % half_frame == 0 and s < UNITS_PER_FRAME:
                 b_next = s // half_frame
                 v_grouped[b_next] = single.tile([P, HEADS, HEAD_DIM, PACK], BF16, name="v_grouped", align_bytes=64)
@@ -284,25 +324,16 @@ def tile_attention2_pa_kernel(tc, q, k, v, w_proj, out):
                     transpose_kq_head(1, x, nc.scalar.copy)
                     group_v_head(1, x)
 
-            if 0 <= s - 2 < UNITS:
-                reciprocal_of_sum(s - 2)
-            if s >= 4 and s % 2 == 0:
-                project((s - 4) // 2)
+            maximum_and_reciprocal(unit_or_none(s), unit_or_none(s - 2))
+            if tile_finished_by(s - 3) is not None:
+                attention_times_v(tile_finished_by(s - 3))
+            if tile_finished_by(s - 4) is not None:
+                project(tile_finished_by(s - 4))
             if s < UNITS:
                 shift_by_maximum(s)
             if s + 1 < UNITS:
                 score_matmuls(s + 1)
+                seed_maximum(s + 1)
             if s < UNITS:
                 exponentials(s)
                 sum_over_heads(s)
-            if s + 1 < UNITS:
-                seed_maximum(s + 1)
-            if s == half_frame - 1:
-                quantise_v(0)
-                quantise_w()
-            if s == UNITS_PER_FRAME - 1:
-                quantise_v(1)
-            if 0 <= s - 2 < UNITS:
-                normalise(s - 2)
-                if s % 2 == 1:
-                    attention_times_v((s - 3) // 2)

@@ -44,12 +44,15 @@ def tile_attention2_pa_kernel(tc, q, k, v, w_proj, out):
         keep = stack.enter_context(tc.tile_pool(name="keep", bufs=1))
         single = stack.enter_context(tc.tile_pool(name="single", bufs=1))
         double = stack.enter_context(tc.tile_pool(name="double", bufs=2))
-        triple = stack.enter_context(tc.tile_pool(name="triple", bufs=3))
+        fourfold = stack.enter_context(tc.tile_pool(name="fourfold", bufs=4))
         score_psum = stack.enter_context(tc.psum_pool(name="score_psum", bufs=1))
-        aux_psum = stack.enter_context(tc.psum_pool(name="aux_psum", bufs=4))
+        recip_psum = stack.enter_context(tc.psum_pool(name="recip_psum", bufs=1))
+        aux_psum = stack.enter_context(tc.psum_pool(name="aux_psum", bufs=3))
 
         identity = const.tile([P, P], BF16)
         make_identity(nc, identity[:])
+        identity_f32 = const.tile([P, P], F32)
+        make_identity(nc, identity_f32[:])
 
         def load_kq(b):
             kq_raw = raw.tile([P, HEADS, 2 * PACK, HEAD_DIM], BF16, name="kq_raw")
@@ -96,7 +99,14 @@ def tile_attention2_pa_kernel(tc, q, k, v, w_proj, out):
             copy_out(out=kqT[b][:, h, :, :], in_=kq_ps[:])
 
         def group_v_head(b, h):
-            nc.scalar.copy(out=v_grouped[b][:, h, :, :], in_=v_raw[b][:, h, :, :].rearrange("p t d -> p d t"))
+            nc.gpsimd.tensor_scalar(
+                out=v_grouped[b][:, h, :, :],
+                in0=v_raw[b][:, h, :, :].rearrange("p t d -> p d t"),
+                scalar1=1.0,
+                scalar2=0.0,
+                op0=ALU.mult,
+                op1=ALU.add,
+            )
 
         def quantise_v(b):
             nc.vector.quantize_mx(
@@ -157,28 +167,34 @@ def tile_attention2_pa_kernel(tc, q, k, v, w_proj, out):
             return s_ps[:].rearrange("p i n t -> p i (n t)")
 
         def seed_maximum(u):
-            run_a = double.tile([P, HEADS_PER_BANK, UNIT_COLS], F32)
-            run_b = double.tile([P, HEADS_PER_BANK, UNIT_COLS], F32)
-            nc.scalar.copy(out=run_a[:], in_=bank_view(scores[u][0]))
-            nc.scalar.copy(out=run_b[:], in_=bank_view(scores[u][1]))
-            running[u] = (run_a, run_b)
+            run = double.tile([P, HEADS_PER_BANK, UNIT_COLS], F32)
+            nc.scalar.copy(out=run[:], in_=bank_view(scores[u][0]))
+            running[u] = run
 
-        def maximum_and_reciprocal(u_max, u_rec):
-            half = UNIT_COLS // 2
-            if u_max is not None:
-                run_a, run_b = running[u_max]
-                nc.vector.tensor_tensor(out=run_a[:], in0=bank_view(scores[u_max][2]), in1=run_a[:], op=ALU.max)
-                nc.vector.tensor_tensor(out=run_b[:], in0=bank_view(scores[u_max][3]), in1=run_b[:], op=ALU.max)
-            if u_rec is not None:
-                recips[u_rec] = double.tile([P, UNIT_COLS], F32, name="r")
-                nc.vector.reciprocal(out=recips[u_rec][:, :half], in_=totals[u_rec][:, :half])
-            if u_max is not None:
-                nc.vector.tensor_tensor(out=run_a[:], in0=run_a[:], in1=run_b[:], op=ALU.max)
-            if u_rec is not None:
-                nc.vector.reciprocal(out=recips[u_rec][:, half:], in_=totals[u_rec][:, half:])
-            if u_max is not None:
-                tops[u_max] = double.tile([P, UNIT_COLS], F32, name="top")
-                nc.vector.tensor_tensor(out=tops[u_max][:], in0=run_a[:, 0, :], in1=run_a[:, 1, :], op=ALU.max)
+        def normalise_heads(u, first, count):
+            m, half = u // 2, u % 2
+            if first == 0 and half == 0:
+                attn[m] = single.tile([P, HEADS, TILE_COLS], BF16, name="attn", align_bytes=64)
+            cols = slice(half * UNIT_COLS, (half + 1) * UNIT_COLS)
+            nc.vector.tensor_tensor(
+                out=attn[m][:, first : first + count, cols],
+                in0=expd[u][:, first : first + count, :],
+                in1=recips[m][:, cols].unsqueeze(1).to_broadcast([P, count, UNIT_COLS]),
+                op=ALU.mult,
+            )
+
+        def maximum_and_normalise(u_max, u_norm):
+            quarter = HEADS // SCORE_BANKS
+            for i in range(SCORE_BANKS):
+                if u_max is not None:
+                    run = running[u_max]
+                    if i + 1 < SCORE_BANKS:
+                        nc.vector.tensor_tensor(out=run[:], in0=bank_view(scores[u_max][i + 1]), in1=run[:], op=ALU.max)
+                    else:
+                        tops[u_max] = double.tile([P, UNIT_COLS], F32, name="top")
+                        nc.vector.tensor_tensor(out=tops[u_max][:], in0=run[:, 0, :], in1=run[:, 1, :], op=ALU.max)
+                if u_norm is not None:
+                    normalise_heads(u_norm, i * quarter, quarter)
 
         def shift_by_maximum(u):
             diff = single.tile([P, HEADS, UNIT_COLS], F32)
@@ -192,37 +208,42 @@ def tile_attention2_pa_kernel(tc, q, k, v, w_proj, out):
             shifted[u] = diff
 
         def exponentials(u):
-            e = triple.tile([P, HEADS, UNIT_COLS], F32)
+            e = fourfold.tile([P, HEADS, UNIT_COLS], F32)
             nc.scalar.activation(out=e[:], in_=shifted[u][:], func=ACT.Exp, scale=HEAD_DIM**-0.5)
             expd[u] = e
 
         def sum_over_heads(u):
+            m, half = u // 2, u % 2
+            if half == 0:
+                totals[m] = double.tile([P, 2, UNIT_COLS], F32, name="total")
             e = expd[u]
             four = single.tile([P, 4, UNIT_COLS], F32)
             two = single.tile([P, 2, UNIT_COLS], F32)
-            total = double.tile([P, UNIT_COLS], F32)
             nc.gpsimd.tensor_tensor(out=four[:], in0=e[:, 0:4, :], in1=e[:, 4:8, :], op=ALU.add)
             nc.gpsimd.tensor_tensor(out=two[:], in0=four[:, 0:2, :], in1=four[:, 2:4, :], op=ALU.add)
-            nc.gpsimd.tensor_tensor(out=total[:], in0=two[:, 0, :], in1=two[:, 1, :], op=ALU.add)
-            totals[u] = total
+            nc.gpsimd.tensor_tensor(out=totals[m][:, half, :], in0=two[:, 0, :], in1=two[:, 1, :], op=ALU.add)
 
-        def normalise(u):
-            m, half = u // 2, u % 2
-            if half == 0:
-                attn[m] = single.tile([P, HEADS, TILE_COLS], BF16, name="attn", align_bytes=64)
-            nc.vector.tensor_tensor(
-                out=attn[m][:, :, half * UNIT_COLS : (half + 1) * UNIT_COLS],
-                in0=expd[u][:],
-                in1=recips[u][:].unsqueeze(1).to_broadcast([P, HEADS, UNIT_COLS]),
-                op=ALU.mult,
-            )
-
+        logs = {}
+        recips_sbuf = {}
+        a_words = {}
         o_banks = {}
         o_grouped = {}
+        o_words = {}
         y_banks = {}
 
-        def attention_times_v(m):
-            b = m // TILES_PER_FRAME
+        def log_of_sums(m):
+            logs[m] = double.tile([P, TILE_COLS], F32, name="log_total")
+            nc.scalar.activation(out=logs[m][:], in_=totals[m][:].rearrange("p u c -> p (u c)"), func=ACT.Ln)
+
+        def reciprocal_of_sums(m):
+            recips_sbuf[m] = double.tile([P, TILE_COLS], F32, name="recip")
+            nc.scalar.activation(out=recips_sbuf[m][:], in_=logs[m][:], func=ACT.Exp, scale=-1.0)
+
+        def reciprocal_to_psum(m):
+            recips[m] = recip_psum.tile([P, TILE_COLS], F32, name="recip_ps")
+            nc.tensor.matmul(out=recips[m][:], lhsT=identity_f32[:], rhs=recips_sbuf[m][:], start=True, stop=True)
+
+        def quantise_attn(m):
             a_codes = double.tile([P, HEADS * TILE_Q], U32, align_bytes=64)
             a_scales = double.tile([P, HEADS * TILE_Q], U8, align_bytes=64)
             nc.vector.quantize_mx(
@@ -230,6 +251,11 @@ def tile_attention2_pa_kernel(tc, q, k, v, w_proj, out):
                 scales=a_scales[:],
                 in_=attn[m][:].rearrange("p h c -> p (h c)"),
             )
+            a_words[m] = (a_codes, a_scales)
+
+        def attention_times_v(m):
+            b = m // TILES_PER_FRAME
+            a_codes, a_scales = a_words[m]
             o_banks[m] = []
             for g in range(PASSES):
                 o_ps = aux_psum.tile([P, PACK, TILE_Q], F32, tag="aux")
@@ -252,7 +278,7 @@ def tile_attention2_pa_kernel(tc, q, k, v, w_proj, out):
             for g, o_ps in enumerate(o_banks[m]):
                 nc.scalar.copy(out=o_grouped[m][:, g, :, :], in_=o_ps[:].rearrange("p t n -> p n t"))
 
-        def project(m):
+        def quantise_o(m):
             o_codes = double.tile([P, PASSES * TILE_Q], U32, align_bytes=64)
             o_scales = double.tile([P, PASSES * TILE_Q], U8, align_bytes=64)
             nc.vector.quantize_mx(
@@ -260,6 +286,10 @@ def tile_attention2_pa_kernel(tc, q, k, v, w_proj, out):
                 scales=o_scales[:],
                 in_=o_grouped[m][:].rearrange("p g n t -> p (g n t)"),
             )
+            o_words[m] = (o_codes, o_scales)
+
+        def project(m):
+            o_codes, o_scales = o_words[m]
             y_banks[m] = []
             for c0 in range(0, C_OUT, BANK):
                 y_ps = aux_psum.tile([P, BANK], F32, tag="aux")
@@ -299,41 +329,51 @@ def tile_attention2_pa_kernel(tc, q, k, v, w_proj, out):
 
         half_frame = UNITS_PER_FRAME // 2
         for s in range(UNITS + 6):
-            if unit_or_none(s - 3) is not None:
-                normalise(s - 3)
-
             if s == half_frame:
                 quantise_v(0)
                 quantise_w()
             if s == UNITS_PER_FRAME:
                 quantise_v(1)
 
-            if tile_finished_by(s - 4) is not None:
-                round_o(tile_finished_by(s - 4))
             if tile_finished_by(s - 5) is not None:
-                store(tile_finished_by(s - 5))
-            if s % half_frame == 0 and s < UNITS_PER_FRAME:
-                b_next = s // half_frame
-                v_grouped[b_next] = single.tile([P, HEADS, HEAD_DIM, PACK], BF16, name="v_grouped", align_bytes=64)
-            if s < half_frame:
-                for x in (2 * s, 2 * s + 1):
-                    group_v_head(0, x)
-                    transpose_w_rows(x)
-            elif s < UNITS_PER_FRAME:
-                for x in (2 * (s - half_frame), 2 * (s - half_frame) + 1):
-                    transpose_kq_head(1, x, nc.scalar.copy)
-                    group_v_head(1, x)
+                round_o(tile_finished_by(s - 5))
+            if s < UNITS_PER_FRAME:
+                b_side, first = divmod(2 * s, HEADS)
+                if first == 0:
+                    v_grouped[b_side] = single.tile([P, HEADS, HEAD_DIM, PACK], BF16, name="v_grouped", align_bytes=64)
+                for x in (first, first + 1):
+                    group_v_head(b_side, x)
+                if s % 2 == 0:
+                    for x in range(first, first + 4):
+                        if b_side == 0:
+                            transpose_w_rows(x)
+                        else:
+                            transpose_kq_head(1, x, nc.scalar.copy)
 
-            maximum_and_reciprocal(unit_or_none(s), unit_or_none(s - 2))
-            if tile_finished_by(s - 3) is not None:
-                attention_times_v(tile_finished_by(s - 3))
-            if tile_finished_by(s - 4) is not None:
-                project(tile_finished_by(s - 4))
+            maximum_and_normalise(unit_or_none(s), unit_or_none(s - 4))
+            if tile_finished_by(s - 2) is not None:
+                reciprocal_to_psum(tile_finished_by(s - 2))
             if s < UNITS:
                 shift_by_maximum(s)
+            if tile_finished_by(s - 4) is not None:
+                quantise_attn(tile_finished_by(s - 4))
+            if tile_finished_by(s - 5) is not None:
+                quantise_o(tile_finished_by(s - 5))
+
             if s + 1 < UNITS:
                 score_matmuls(s + 1)
                 seed_maximum(s + 1)
+            if tile_finished_by(s - 6) is not None:
+                store(tile_finished_by(s - 6))
+            if tile_finished_by(s - 4) is not None:
+                attention_times_v(tile_finished_by(s - 4))
+            if tile_finished_by(s - 5) is not None:
+                project(tile_finished_by(s - 5))
+            if tile_finished_by(s - 1) is not None:
+                log_of_sums(tile_finished_by(s - 1))
             if s < UNITS:
                 exponentials(s)
+            if tile_finished_by(s - 1) is not None:
+                reciprocal_of_sums(tile_finished_by(s - 1))
+            if s < UNITS:
                 sum_over_heads(s)

@@ -144,12 +144,13 @@ def tile_attention2_pa_kernel(tc, q, k, v, w_proj, out):
         def frame_of(u):
             return u // UNITS_PER_FRAME
 
-        def score_matmuls(u):
+        def score_matmuls(u, banks):
             b = frame_of(u)
             first = (u % UNITS_PER_FRAME) * CHUNK
             j, col = first // P, first % P
-            scores[u] = []
-            for bank in range(SCORE_BANKS):
+            if u not in scores:
+                scores[u] = []
+            for bank in banks:
                 s_ps = score_psum.tile([P, HEADS_PER_BANK, CHUNK, PACK], F32, name="s_ps%d" % bank)
                 for i in range(HEADS_PER_BANK):
                     h = bank * HEADS_PER_BANK + i
@@ -307,12 +308,13 @@ def tile_attention2_pa_kernel(tc, q, k, v, w_proj, out):
                     )
                 y_banks[m].append(y_ps)
 
-        def store(m):
+        def store(m, i):
             b, j = divmod(m, TILES_PER_FRAME)
-            y = double.tile([P, C_OUT], F32)
-            for i, y_ps in enumerate(y_banks[m]):
-                nc.scalar.copy(out=y[:, i * BANK : (i + 1) * BANK], in_=y_ps[:])
-            nc.sync.dma_start(out=out[b].rearrange("(p j) c -> p j c", j=PACK)[:, j, :], in_=y[:])
+            y = double.tile([P, BANK], F32)
+            nc.scalar.copy(out=y[:], in_=y_banks[m][i][:])
+            nc.sync.dma_start(
+                out=out[b].rearrange("(p j) c -> p j c", j=PACK)[:, j, i * BANK : (i + 1) * BANK], in_=y[:]
+            )
 
         def unit_or_none(u):
             return u if 0 <= u < UNITS else None
@@ -324,17 +326,22 @@ def tile_attention2_pa_kernel(tc, q, k, v, w_proj, out):
             transpose_kq_head(0, h, nc.scalar.copy if h % 2 == 0 else nc.vector.tensor_copy)
         kq_raw[1] = load_kq(1)
         v_raw[1] = load_v(1)
-        score_matmuls(0)
+        score_matmuls(0, range(SCORE_BANKS))
         seed_maximum(0)
 
         half_frame = UNITS_PER_FRAME // 2
-        for s in range(UNITS + 6):
+        for s in range(UNITS + 7):
             if s == half_frame:
                 quantise_v(0)
                 quantise_w()
             if s == UNITS_PER_FRAME:
                 quantise_v(1)
 
+            if tile_finished_by(s - 2) is not None:
+                log_of_sums(tile_finished_by(s - 2))
+                reciprocal_of_sums(tile_finished_by(s - 2))
+            if tile_finished_by(s - 7) is not None:
+                store(tile_finished_by(s - 7), 1)
             if tile_finished_by(s - 5) is not None:
                 round_o(tile_finished_by(s - 5))
             if s < UNITS_PER_FRAME:
@@ -351,8 +358,6 @@ def tile_attention2_pa_kernel(tc, q, k, v, w_proj, out):
                             transpose_kq_head(1, x, nc.scalar.copy)
 
             maximum_and_normalise(unit_or_none(s), unit_or_none(s - 4))
-            if tile_finished_by(s - 2) is not None:
-                reciprocal_to_psum(tile_finished_by(s - 2))
             if s < UNITS:
                 shift_by_maximum(s)
             if tile_finished_by(s - 4) is not None:
@@ -361,19 +366,18 @@ def tile_attention2_pa_kernel(tc, q, k, v, w_proj, out):
                 quantise_o(tile_finished_by(s - 5))
 
             if s + 1 < UNITS:
-                score_matmuls(s + 1)
+                score_matmuls(s + 1, (0, 1))
                 seed_maximum(s + 1)
+            if tile_finished_by(s - 2) is not None:
+                reciprocal_to_psum(tile_finished_by(s - 2))
+            if s + 1 < UNITS:
+                score_matmuls(s + 1, (2, 3))
             if tile_finished_by(s - 6) is not None:
-                store(tile_finished_by(s - 6))
+                store(tile_finished_by(s - 6), 0)
             if tile_finished_by(s - 4) is not None:
                 attention_times_v(tile_finished_by(s - 4))
             if tile_finished_by(s - 5) is not None:
                 project(tile_finished_by(s - 5))
-            if tile_finished_by(s - 1) is not None:
-                log_of_sums(tile_finished_by(s - 1))
             if s < UNITS:
                 exponentials(s)
-            if tile_finished_by(s - 1) is not None:
-                reciprocal_of_sums(tile_finished_by(s - 1))
-            if s < UNITS:
                 sum_over_heads(s)

@@ -144,13 +144,12 @@ def tile_attention2_pa_kernel(tc, q, k, v, w_proj, out):
         def frame_of(u):
             return u // UNITS_PER_FRAME
 
-        def score_matmuls(u, banks):
+        def score_matmuls(u):
             b = frame_of(u)
             first = (u % UNITS_PER_FRAME) * CHUNK
             j, col = first // P, first % P
-            if u not in scores:
-                scores[u] = []
-            for bank in banks:
+            scores[u] = []
+            for bank in range(SCORE_BANKS):
                 s_ps = score_psum.tile([P, HEADS_PER_BANK, CHUNK, PACK], F32, name="s_ps%d" % bank)
                 for i in range(HEADS_PER_BANK):
                     h = bank * HEADS_PER_BANK + i
@@ -185,7 +184,6 @@ def tile_attention2_pa_kernel(tc, q, k, v, w_proj, out):
             )
 
         def maximum_and_normalise(u_max, u_norm):
-            quarter = HEADS // SCORE_BANKS
             for i in range(SCORE_BANKS):
                 if u_max is not None:
                     run = running[u_max]
@@ -195,7 +193,7 @@ def tile_attention2_pa_kernel(tc, q, k, v, w_proj, out):
                         tops[u_max] = double.tile([P, UNIT_COLS], F32, name="top")
                         nc.vector.tensor_tensor(out=tops[u_max][:], in0=run[:, 0, :], in1=run[:, 1, :], op=ALU.max)
                 if u_norm is not None:
-                    normalise_heads(u_norm, i * quarter, quarter)
+                    normalise_heads(u_norm, i, 1)
 
         def shift_by_maximum(u):
             diff = single.tile([P, HEADS, UNIT_COLS], F32)
@@ -326,7 +324,7 @@ def tile_attention2_pa_kernel(tc, q, k, v, w_proj, out):
             transpose_kq_head(0, h, nc.scalar.copy if h % 2 == 0 else nc.vector.tensor_copy)
         kq_raw[1] = load_kq(1)
         v_raw[1] = load_v(1)
-        score_matmuls(0, range(SCORE_BANKS))
+        score_matmuls(0)
         seed_maximum(0)
 
         half_frame = UNITS_PER_FRAME // 2
@@ -360,18 +358,18 @@ def tile_attention2_pa_kernel(tc, q, k, v, w_proj, out):
             maximum_and_normalise(unit_or_none(s), unit_or_none(s - 4))
             if s < UNITS:
                 shift_by_maximum(s)
+            if unit_or_none(s - 4) is not None:
+                normalise_heads(s - 4, SCORE_BANKS, HEADS - SCORE_BANKS)
             if tile_finished_by(s - 4) is not None:
                 quantise_attn(tile_finished_by(s - 4))
             if tile_finished_by(s - 5) is not None:
                 quantise_o(tile_finished_by(s - 5))
 
             if s + 1 < UNITS:
-                score_matmuls(s + 1, (0, 1))
+                score_matmuls(s + 1)
                 seed_maximum(s + 1)
             if tile_finished_by(s - 2) is not None:
                 reciprocal_to_psum(tile_finished_by(s - 2))
-            if s + 1 < UNITS:
-                score_matmuls(s + 1, (2, 3))
             if tile_finished_by(s - 6) is not None:
                 store(tile_finished_by(s - 6), 0)
             if tile_finished_by(s - 4) is not None:

@@ -31,6 +31,8 @@ SCORE_BANKS = HEADS // HEADS_PER_BANK
 TILE_Q = 128
 TILE_COLS = TILE_Q * PACK
 TILES_PER_FRAME = TOKENS // TILE_Q
+GPSIMD_HEADS = 2
+VECTOR_HEADS = HEADS - GPSIMD_HEADS
 
 FLOPS = 2 * FRAMES * HEADS * TOKENS * TOKENS * HEAD_DIM * 2 + 2 * FRAMES * TOKENS * CHANNELS * C_OUT
 
@@ -144,12 +146,13 @@ def tile_attention2_pa_kernel(tc, q, k, v, w_proj, out):
         def frame_of(u):
             return u // UNITS_PER_FRAME
 
-        def score_matmuls(u):
+        def score_matmuls(u, banks):
             b = frame_of(u)
             first = (u % UNITS_PER_FRAME) * CHUNK
             j, col = first // P, first % P
-            scores[u] = []
-            for bank in range(SCORE_BANKS):
+            if u not in scores:
+                scores[u] = []
+            for bank in banks:
                 s_ps = score_psum.tile([P, HEADS_PER_BANK, CHUNK, PACK], F32, name="s_ps%d" % bank)
                 for i in range(HEADS_PER_BANK):
                     h = bank * HEADS_PER_BANK + i
@@ -171,15 +174,27 @@ def tile_attention2_pa_kernel(tc, q, k, v, w_proj, out):
             nc.scalar.copy(out=run[:], in_=bank_view(scores[u][0]))
             running[u] = run
 
-        def normalise_heads(u, first, count):
+        def normalise_on_gpsimd(u):
             m, half = u // 2, u % 2
-            if first == 0 and half == 0:
+            if half == 0:
                 attn[m] = single.tile([P, HEADS, TILE_COLS], BF16, name="attn", align_bytes=64)
             cols = slice(half * UNIT_COLS, (half + 1) * UNIT_COLS)
+            nc.gpsimd.tensor_tensor(
+                out=attn[m][:, VECTOR_HEADS:, cols],
+                in0=expd[u][:, VECTOR_HEADS:, :],
+                in1=recips_sbuf[m][:, cols].unsqueeze(1).to_broadcast([P, GPSIMD_HEADS, UNIT_COLS]),
+                op=ALU.mult,
+            )
+
+        def normalise_on_vector(u, piece):
+            m, half = u // 2, u % 2
+            width = UNIT_COLS // SCORE_BANKS
+            unit_cols = slice(piece * width, (piece + 1) * width)
+            tile_cols = slice(half * UNIT_COLS + piece * width, half * UNIT_COLS + (piece + 1) * width)
             nc.vector.tensor_tensor(
-                out=attn[m][:, first : first + count, cols],
-                in0=expd[u][:, first : first + count, :],
-                in1=recips[m][:, cols].unsqueeze(1).to_broadcast([P, count, UNIT_COLS]),
+                out=attn[m][:, :VECTOR_HEADS, tile_cols],
+                in0=expd[u][:, :VECTOR_HEADS, unit_cols],
+                in1=recips[m][:, tile_cols].unsqueeze(1).to_broadcast([P, VECTOR_HEADS, width]),
                 op=ALU.mult,
             )
 
@@ -193,7 +208,7 @@ def tile_attention2_pa_kernel(tc, q, k, v, w_proj, out):
                         tops[u_max] = double.tile([P, UNIT_COLS], F32, name="top")
                         nc.vector.tensor_tensor(out=tops[u_max][:], in0=run[:, 0, :], in1=run[:, 1, :], op=ALU.max)
                 if u_norm is not None:
-                    normalise_heads(u_norm, i, 1)
+                    normalise_on_vector(u_norm, i)
 
         def shift_by_maximum(u):
             diff = single.tile([P, HEADS, UNIT_COLS], F32)
@@ -324,14 +339,15 @@ def tile_attention2_pa_kernel(tc, q, k, v, w_proj, out):
             transpose_kq_head(0, h, nc.scalar.copy if h % 2 == 0 else nc.vector.tensor_copy)
         kq_raw[1] = load_kq(1)
         v_raw[1] = load_v(1)
-        score_matmuls(0)
+        score_matmuls(0, range(SCORE_BANKS))
         seed_maximum(0)
 
         half_frame = UNITS_PER_FRAME // 2
         for s in range(UNITS + 7):
+            if s == half_frame - 1:
+                quantise_w()
             if s == half_frame:
                 quantise_v(0)
-                quantise_w()
             if s == UNITS_PER_FRAME:
                 quantise_v(1)
 
@@ -358,24 +374,26 @@ def tile_attention2_pa_kernel(tc, q, k, v, w_proj, out):
             maximum_and_normalise(unit_or_none(s), unit_or_none(s - 4))
             if s < UNITS:
                 shift_by_maximum(s)
-            if unit_or_none(s - 4) is not None:
-                normalise_heads(s - 4, SCORE_BANKS, HEADS - SCORE_BANKS)
             if tile_finished_by(s - 4) is not None:
                 quantise_attn(tile_finished_by(s - 4))
             if tile_finished_by(s - 5) is not None:
                 quantise_o(tile_finished_by(s - 5))
 
             if s + 1 < UNITS:
-                score_matmuls(s + 1)
+                score_matmuls(s + 1, (0, 1))
                 seed_maximum(s + 1)
             if tile_finished_by(s - 2) is not None:
                 reciprocal_to_psum(tile_finished_by(s - 2))
+            if s + 1 < UNITS:
+                score_matmuls(s + 1, (2, 3))
             if tile_finished_by(s - 6) is not None:
                 store(tile_finished_by(s - 6), 0)
             if tile_finished_by(s - 4) is not None:
                 attention_times_v(tile_finished_by(s - 4))
             if tile_finished_by(s - 5) is not None:
                 project(tile_finished_by(s - 5))
+            if unit_or_none(s - 3) is not None:
+                normalise_on_gpsimd(s - 3)
             if s < UNITS:
                 exponentials(s)
                 sum_over_heads(s)

@@ -31,10 +31,13 @@ SCORE_BANKS = HEADS // HEADS_PER_BANK
 TILE_Q = 128
 TILE_COLS = TILE_Q * PACK
 TILES_PER_FRAME = TOKENS // TILE_Q
-GPSIMD_HEADS = 2
-VECTOR_HEADS = HEADS - GPSIMD_HEADS
 
 FLOPS = 2 * FRAMES * HEADS * TOKENS * TOKENS * HEAD_DIM * 2 + 2 * FRAMES * TOKENS * CHANNELS * C_OUT
+
+
+SUM_BLOCKS = UNIT_COLS // P
+LAST_TILE = UNITS // 2 - 1
+SHARED_TILES = LAST_TILE - 1
 
 
 def tile_attention2_pa_kernel(tc, q, k, v, w_proj, out):
@@ -43,64 +46,102 @@ def tile_attention2_pa_kernel(tc, q, k, v, w_proj, out):
         stack.enter_context(tc.manual_schedule())
         const = stack.enter_context(tc.tile_pool(name="const", bufs=1))
         raw = stack.enter_context(tc.tile_pool(name="raw", bufs=1))
+        raw2 = stack.enter_context(tc.tile_pool(name="raw2", bufs=2))
         keep = stack.enter_context(tc.tile_pool(name="keep", bufs=1))
         single = stack.enter_context(tc.tile_pool(name="single", bufs=1))
         double = stack.enter_context(tc.tile_pool(name="double", bufs=2))
-        fourfold = stack.enter_context(tc.tile_pool(name="fourfold", bufs=4))
+        deep = stack.enter_context(tc.tile_pool(name="deep", bufs=7))
         score_psum = stack.enter_context(tc.psum_pool(name="score_psum", bufs=1))
-        recip_psum = stack.enter_context(tc.psum_pool(name="recip_psum", bufs=1))
+        sum_psum = stack.enter_context(tc.psum_pool(name="sum_psum", bufs=1))
         aux_psum = stack.enter_context(tc.psum_pool(name="aux_psum", bufs=3))
+
+        def rows_by_four(src):
+            return src.rearrange("h (p x) d -> p h x d", x=PACK)
+
+        k_raw = {}
+        q_raw = {}
+        v_raw = {}
+
+        def load_k(b, pieces):
+            k_raw[b] = raw.tile([P, HEADS, PACK, HEAD_DIM], BF16, name="k_raw")
+            width = HEADS // pieces
+            for h0 in range(0, HEADS, width):
+                nc.sync.dma_start(
+                    out=k_raw[b][:, h0 : h0 + width].rearrange("p h x d -> p h (x d)"),
+                    in_=k[b, h0 : h0 + width].rearrange("h (p x) d -> p h (x d)", x=PACK),
+                )
+
+        def load_q(b, j0, j1):
+            if j0 == 0:
+                q_raw[b] = raw2.tile([P, HEADS, PACK, HEAD_DIM], BF16, name="q_raw")
+            nc.sync.dma_start(
+                out=q_raw[b][:, :, j0:j1, :].rearrange("p h x d -> p h (x d)"),
+                in_=q[b].rearrange("h (p x) d -> p h (x d)", x=PACK)[:, :, j0 * HEAD_DIM : j1 * HEAD_DIM],
+            )
+
+        def load_v(b):
+            v_raw[b] = raw.tile([P, HEADS, PACK, HEAD_DIM], BF16, name="v_raw")
+            nc.sync.dma_start(
+                out=v_raw[b][:].rearrange("p h t d -> p h (t d)"),
+                in_=v[b].rearrange("h (p t) d -> p h (t d)", t=PACK),
+            )
+
+        w_raw = raw.tile([P, C_OUT // P, CHANNELS], BF16)
+
+        def load_w():
+            w_rows = w_proj.rearrange("(i p) c -> p i c", p=P)
+            for i0 in (0, 4):
+                nc.sync.dma_start(out=w_raw[:, i0 : i0 + 4, :], in_=w_rows[:, i0 : i0 + 4, :])
+
+        load_q(0, 0, 1)
+        load_k(0, 4)
+        load_q(0, 1, PACK)
+        load_v(0)
+        load_w()
 
         identity = const.tile([P, P], BF16)
         make_identity(nc, identity[:])
         identity_f32 = const.tile([P, P], F32)
         make_identity(nc, identity_f32[:])
 
-        def load_kq(b):
-            kq_raw = raw.tile([P, HEADS, 2 * PACK, HEAD_DIM], BF16, name="kq_raw")
-            half = HEADS // 2
-            for h0 in (0, half):
-                for x0, src in ((0, k), (PACK, q)):
-                    nc.sync.dma_start(
-                        out=kq_raw[:, h0 : h0 + half, x0 : x0 + PACK, :].rearrange("p h x d -> p h (x d)"),
-                        in_=src[b, h0 : h0 + half].rearrange("h (p x) d -> p h (x d)", x=PACK),
-                    )
-            return kq_raw
-
-        def load_v(b):
-            v_raw = raw.tile([P, HEADS, PACK, HEAD_DIM], BF16, name="v_raw%d" % b)
-            nc.sync.dma_start(
-                out=v_raw[:].rearrange("p h t d -> p h (t d)"),
-                in_=v[b].rearrange("h (p t) d -> p h (t d)", t=PACK),
-            )
-            return v_raw
-
-        kq_raw = {0: load_kq(0)}
-        w_raw = raw.tile([P, C_OUT // P, CHANNELS], BF16)
-        w_rows = w_proj.rearrange("(i p) c -> p i c", p=P)
-        for i0 in (0, 4):
-            nc.sync.dma_start(out=w_raw[:, i0 : i0 + 4, :], in_=w_rows[:, i0 : i0 + 4, :])
-        v_raw = {0: load_v(0)}
-
-        kqT = {}
+        kT = {}
+        qT = {}
         v_grouped = {}
         v_codes = {}
         v_scales = {}
         for b in range(FRAMES):
-            kqT[b] = keep.tile([P, HEADS, 2 * PACK, P], BF16, name="kqT%d" % b)
+            kT[b] = keep.tile([P, HEADS, PACK, P], BF16, name="kT%d" % b)
+            qT[b] = keep.tile([P, PACK, HEADS, P], BF16, name="qT%d" % b)
             v_codes[b] = keep.tile([P, HEADS * HEAD_DIM], U32, name="v_codes%d" % b, align_bytes=64)
             v_scales[b] = keep.tile([P, HEADS * HEAD_DIM], U8, name="v_scales%d" % b, align_bytes=64)
         w_grouped = keep.tile([P, PASSES, C_OUT, PACK], BF16, align_bytes=64)
         w_codes = keep.tile([P, PASSES * C_OUT], U32, align_bytes=64)
         w_scales = keep.tile([P, PASSES * C_OUT], U8, align_bytes=64)
 
-        def transpose_kq_head(b, h, copy_out):
-            kq_ps = aux_psum.tile([P, 2 * PACK, P], BF16, tag="aux")
-            for x in range(2 * PACK):
-                nc.tensor.transpose(kq_ps[:, x, :], kq_raw[b][:, h, x, :], identity[:])
-            copy_out(out=kqT[b][:, h, :, :], in_=kq_ps[:])
+        turned = {}
+
+        def transpose_k(b, pair):
+            ps = aux_psum.tile([P, 2, PACK, P], BF16, tag="aux", name="k_ps")
+            for i in range(2):
+                for t in range(PACK):
+                    nc.tensor.transpose(ps[:, i, t, :], k_raw[b][:, 2 * pair + i, t, :], identity[:])
+            turned["k", b, pair] = ps
+
+        def copy_k(b, pair, copy):
+            copy(out=kT[b][:, 2 * pair : 2 * pair + 2, :, :], in_=turned["k", b, pair][:])
+
+        def transpose_q(b, j):
+            ps = aux_psum.tile([P, HEADS, P], BF16, tag="aux", name="q_ps")
+            for h in range(HEADS):
+                nc.tensor.transpose(ps[:, h, :], q_raw[b][:, h, j, :], identity[:])
+            turned["q", b, j] = ps
+
+        def copy_q(b, j, copy):
+            copy(out=qT[b][:, j, :, :], in_=turned["q", b, j][:])
 
         def group_v_head(b, h):
+            if h == 0:
+                v_grouped[b] = single.tile([P, HEADS, HEAD_DIM, PACK], BF16, name="v_grouped", align_bytes=64)
             nc.gpsimd.tensor_scalar(
                 out=v_grouped[b][:, h, :, :],
                 in0=v_raw[b][:, h, :, :].rearrange("p t d -> p d t"),
@@ -117,128 +158,105 @@ def tile_attention2_pa_kernel(tc, q, k, v, w_proj, out):
                 in_=v_grouped[b][:].rearrange("p h d t -> p (h d t)"),
             )
 
-        def transpose_w_rows(i):
-            w_ps = aux_psum.tile([P, PASSES * PACK, P], BF16, tag="aux")
+        def transpose_w(i):
+            ps = aux_psum.tile([P, PASSES * PACK, P], BF16, tag="aux", name="w_ps")
             for c in range(PASSES * PACK):
-                nc.tensor.transpose(w_ps[:, c, :], w_raw[:, i, c * P : (c + 1) * P], identity[:])
-            nc.scalar.copy(
+                nc.tensor.transpose(ps[:, c, :], w_raw[:, i, c * P : (c + 1) * P], identity[:])
+            turned["w", i] = ps
+
+        def copy_w(i, copy):
+            copy(
                 out=w_grouped[:, :, i * P : (i + 1) * P, :],
-                in_=w_ps[:].rearrange("p (g t) r -> p g r t", t=PACK),
+                in_=turned["w", i][:].rearrange("p (g t) r -> p g r t", t=PACK),
             )
 
-        def quantise_w():
-            for g in range(PASSES):
-                nc.vector.quantize_mx(
-                    out=w_codes[:, g * C_OUT : (g + 1) * C_OUT].bitcast(FP8X4),
-                    scales=w_scales[:, g * C_OUT : (g + 1) * C_OUT],
-                    in_=w_grouped[:, g, :, :].rearrange("p r t -> p (r t)"),
-                )
+        def quantise_w(g):
+            nc.vector.quantize_mx(
+                out=w_codes[:, g * C_OUT : (g + 1) * C_OUT].bitcast(FP8X4),
+                scales=w_scales[:, g * C_OUT : (g + 1) * C_OUT],
+                in_=w_grouped[:, g, :, :].rearrange("p r t -> p (r t)"),
+            )
 
         scores = {}
         running = {}
         tops = {}
-        shifted = {}
         expd = {}
         totals = {}
-        recips = {}
-        attn = {}
 
         def frame_of(u):
             return u // UNITS_PER_FRAME
 
-        def score_matmuls(u, banks):
+        def score_matmuls(u, bank):
             b = frame_of(u)
             first = (u % UNITS_PER_FRAME) * CHUNK
             j, col = first // P, first % P
-            if u not in scores:
+            if bank == 0:
                 scores[u] = []
-            for bank in banks:
-                s_ps = score_psum.tile([P, HEADS_PER_BANK, CHUNK, PACK], F32, name="s_ps%d" % bank)
-                for i in range(HEADS_PER_BANK):
-                    h = bank * HEADS_PER_BANK + i
-                    for t in range(PACK):
-                        nc.tensor.matmul(
-                            out=s_ps[:, i, :, t],
-                            lhsT=kqT[b][:, h, t, :],
-                            rhs=kqT[b][:, h, PACK + j, col : col + CHUNK],
-                            start=True,
-                            stop=True,
-                        )
-                scores[u].append(s_ps)
+            s_ps = score_psum.tile([P, HEADS_PER_BANK, PACK, CHUNK], F32, name="s_ps%d" % bank)
+            for i in range(HEADS_PER_BANK):
+                h = bank * HEADS_PER_BANK + i
+                for t in range(PACK):
+                    nc.tensor.matmul(
+                        out=s_ps[:, i, t, :],
+                        lhsT=kT[b][:, h, t, :],
+                        rhs=qT[b][:, j, h, col : col + CHUNK],
+                        start=True,
+                        stop=True,
+                    )
+            scores[u].append(s_ps)
 
         def bank_view(s_ps):
-            return s_ps[:].rearrange("p i n t -> p i (n t)")
+            return s_ps[:].rearrange("p i t n -> p i n t")
 
         def seed_maximum(u):
-            run = double.tile([P, HEADS_PER_BANK, UNIT_COLS], F32)
-            nc.scalar.copy(out=run[:], in_=bank_view(scores[u][0]))
-            running[u] = run
+            running[u] = double.tile([P, HEADS_PER_BANK, CHUNK, PACK], F32, name="run")
+            nc.scalar.copy(out=running[u][:], in_=bank_view(scores[u][0]))
 
-        def normalise_on_gpsimd(u):
-            m, half = u // 2, u % 2
-            if half == 0:
-                attn[m] = single.tile([P, HEADS, TILE_COLS], BF16, name="attn", align_bytes=64)
-            cols = slice(half * UNIT_COLS, (half + 1) * UNIT_COLS)
-            nc.gpsimd.tensor_tensor(
-                out=attn[m][:, VECTOR_HEADS:, cols],
-                in0=expd[u][:, VECTOR_HEADS:, :],
-                in1=recips_sbuf[m][:, cols].unsqueeze(1).to_broadcast([P, GPSIMD_HEADS, UNIT_COLS]),
-                op=ALU.mult,
-            )
-
-        def normalise_on_vector(u, piece):
-            m, half = u // 2, u % 2
-            width = UNIT_COLS // SCORE_BANKS
-            unit_cols = slice(piece * width, (piece + 1) * width)
-            tile_cols = slice(half * UNIT_COLS + piece * width, half * UNIT_COLS + (piece + 1) * width)
-            nc.vector.tensor_tensor(
-                out=attn[m][:, :VECTOR_HEADS, tile_cols],
-                in0=expd[u][:, :VECTOR_HEADS, unit_cols],
-                in1=recips[m][:, tile_cols].unsqueeze(1).to_broadcast([P, VECTOR_HEADS, width]),
-                op=ALU.mult,
-            )
-
-        def maximum_and_normalise(u_max, u_norm):
-            for i in range(SCORE_BANKS):
-                if u_max is not None:
-                    run = running[u_max]
-                    if i + 1 < SCORE_BANKS:
-                        nc.vector.tensor_tensor(out=run[:], in0=bank_view(scores[u_max][i + 1]), in1=run[:], op=ALU.max)
-                    else:
-                        tops[u_max] = double.tile([P, UNIT_COLS], F32, name="top")
-                        nc.vector.tensor_tensor(out=tops[u_max][:], in0=run[:, 0, :], in1=run[:, 1, :], op=ALU.max)
-                if u_norm is not None:
-                    normalise_on_vector(u_norm, i)
-
-        def shift_by_maximum(u):
-            diff = single.tile([P, HEADS, UNIT_COLS], F32)
-            for bank, s_ps in enumerate(scores[u]):
+        def maximum_step(u, bank):
+            run = running[u]
+            for i in range(HEADS_PER_BANK):
                 nc.vector.tensor_tensor(
-                    out=diff[:, bank * HEADS_PER_BANK : (bank + 1) * HEADS_PER_BANK, :],
-                    in0=bank_view(s_ps),
-                    in1=tops[u][:].unsqueeze(1).to_broadcast([P, HEADS_PER_BANK, UNIT_COLS]),
-                    op=ALU.subtract,
+                    out=run[:, i], in0=scores[u][bank][:, i].rearrange("p t n -> p n t"), in1=run[:, i], op=ALU.max
                 )
-            shifted[u] = diff
+
+        def maximum_end(u):
+            tops[u] = double.tile([P, CHUNK, PACK], F32, name="top")
+            nc.vector.tensor_tensor(out=tops[u][:], in0=running[u][:, 0], in1=running[u][:, 1], op=ALU.max)
+
+        def shift_bank(u, bank):
+            if bank == 0:
+                expd[u] = deep.tile([P, HEADS, UNIT_COLS], F32, name="e")
+            h0 = bank * HEADS_PER_BANK
+            nc.vector.tensor_tensor(
+                out=expd[u][:, h0 : h0 + HEADS_PER_BANK, :].rearrange("p i (n t) -> p i n t", t=PACK),
+                in0=bank_view(scores[u][bank]),
+                in1=tops[u][:].unsqueeze(1).to_broadcast([P, HEADS_PER_BANK, CHUNK, PACK]),
+                op=ALU.subtract,
+            )
 
         def exponentials(u):
-            e = fourfold.tile([P, HEADS, UNIT_COLS], F32)
-            nc.scalar.activation(out=e[:], in_=shifted[u][:], func=ACT.Exp, scale=HEAD_DIM**-0.5)
-            expd[u] = e
+            nc.scalar.activation(out=expd[u][:], in_=expd[u][:], func=ACT.Exp, scale=HEAD_DIM**-0.5)
 
         def sum_over_heads(u):
             m, half = u // 2, u % 2
             if half == 0:
-                totals[m] = double.tile([P, 2, UNIT_COLS], F32, name="total")
-            e = expd[u]
-            four = single.tile([P, 4, UNIT_COLS], F32)
-            two = single.tile([P, 2, UNIT_COLS], F32)
-            nc.gpsimd.tensor_tensor(out=four[:], in0=e[:, 0:4, :], in1=e[:, 4:8, :], op=ALU.add)
-            nc.gpsimd.tensor_tensor(out=two[:], in0=four[:, 0:2, :], in1=four[:, 2:4, :], op=ALU.add)
-            nc.gpsimd.tensor_tensor(out=totals[m][:, half, :], in0=two[:, 0, :], in1=two[:, 1, :], op=ALU.add)
+                totals[m] = sum_psum.tile([P, 2 * SUM_BLOCKS, P], F32, name="total")
+            for i in range(SUM_BLOCKS):
+                for h in range(HEADS):
+                    nc.tensor.matmul(
+                        out=totals[m][:, half * SUM_BLOCKS + i, :],
+                        lhsT=expd[u][:, h, i * P : (i + 1) * P],
+                        rhs=identity_f32[:],
+                        start=(h == 0),
+                        stop=(h == HEADS - 1),
+                        is_transpose=True,
+                    )
 
         logs = {}
-        recips_sbuf = {}
+        recips_t = {}
+        recips_ps = {}
+        recips = {}
+        attn = {}
         a_words = {}
         o_banks = {}
         o_grouped = {}
@@ -247,15 +265,36 @@ def tile_attention2_pa_kernel(tc, q, k, v, w_proj, out):
 
         def log_of_sums(m):
             logs[m] = double.tile([P, TILE_COLS], F32, name="log_total")
-            nc.scalar.activation(out=logs[m][:], in_=totals[m][:].rearrange("p u c -> p (u c)"), func=ACT.Ln)
+            nc.scalar.activation(out=logs[m][:], in_=totals[m][:].rearrange("c i p -> c (i p)"), func=ACT.Ln)
 
         def reciprocal_of_sums(m):
-            recips_sbuf[m] = double.tile([P, TILE_COLS], F32, name="recip")
-            nc.scalar.activation(out=recips_sbuf[m][:], in_=logs[m][:], func=ACT.Exp, scale=-1.0)
+            recips_t[m] = double.tile([P, TILE_COLS], F32, name="recip_t")
+            nc.scalar.activation(out=recips_t[m][:], in_=logs[m][:], func=ACT.Exp, scale=-1.0)
 
-        def reciprocal_to_psum(m):
-            recips[m] = recip_psum.tile([P, TILE_COLS], F32, name="recip_ps")
-            nc.tensor.matmul(out=recips[m][:], lhsT=identity_f32[:], rhs=recips_sbuf[m][:], start=True, stop=True)
+        def turn_reciprocals(m):
+            if m < SHARED_TILES:
+                recips_ps[m] = aux_psum.tile([P, TILE_COLS], F32, tag="aux", name="recip_ps")
+            else:
+                recips_ps[m] = score_psum.tile([P, TILE_COLS], F32, name="s_ps%d" % (m - SHARED_TILES))
+            for i in range(TILE_COLS // P):
+                cols = slice(i * P, (i + 1) * P)
+                nc.tensor.transpose(recips_ps[m][:, cols], recips_t[m][:, cols], identity_f32[:])
+
+        def copy_reciprocals(m, copy):
+            recips[m] = double.tile([P, TILE_COLS], F32, name="recip")
+            copy(out=recips[m][:], in_=recips_ps[m][:])
+
+        def normalise(u, engine, h0, h1, factors):
+            m, half = u // 2, u % 2
+            if m not in attn:
+                attn[m] = double.tile([P, HEADS, TILE_COLS], BF16, name="attn", align_bytes=64)
+            cols = slice(half * UNIT_COLS, (half + 1) * UNIT_COLS)
+            engine.tensor_tensor(
+                out=attn[m][:, h0:h1, cols],
+                in0=expd[u][:, h0:h1, :],
+                in1=factors[:, cols].unsqueeze(1).to_broadcast([P, h1 - h0, UNIT_COLS]),
+                op=ALU.mult,
+            )
 
         def quantise_attn(m):
             a_codes = double.tile([P, HEADS * TILE_Q], U32, align_bytes=64)
@@ -287,10 +326,10 @@ def tile_attention2_pa_kernel(tc, q, k, v, w_proj, out):
                     )
                 o_banks[m].append(o_ps)
 
-        def round_o(m):
-            o_grouped[m] = double.tile([P, PASSES, TILE_Q, PACK], BF16, name="o_grouped", align_bytes=64)
-            for g, o_ps in enumerate(o_banks[m]):
-                nc.scalar.copy(out=o_grouped[m][:, g, :, :], in_=o_ps[:].rearrange("p t n -> p n t"))
+        def round_o(m, g, copy):
+            if g == 0:
+                o_grouped[m] = double.tile([P, PASSES, TILE_Q, PACK], BF16, name="o_grouped", align_bytes=64)
+            copy(out=o_grouped[m][:, g, :, :], in_=o_banks[m][g][:].rearrange("p t n -> p n t"))
 
         def quantise_o(m):
             o_codes = double.tile([P, PASSES * TILE_Q], U32, align_bytes=64)
@@ -321,79 +360,130 @@ def tile_attention2_pa_kernel(tc, q, k, v, w_proj, out):
                     )
                 y_banks[m].append(y_ps)
 
-        def store(m, i):
+        def store(m, i, copy):
             b, j = divmod(m, TILES_PER_FRAME)
-            y = double.tile([P, BANK], F32)
-            nc.scalar.copy(out=y[:], in_=y_banks[m][i][:])
+            y = double.tile([P, BANK], F32, name="y%d" % i)
+            copy(out=y[:], in_=y_banks[m][i][:])
             nc.sync.dma_start(
                 out=out[b].rearrange("(p j) c -> p j c", j=PACK)[:, j, i * BANK : (i + 1) * BANK], in_=y[:]
             )
 
-        def unit_or_none(u):
-            return u if 0 <= u < UNITS else None
+        def unit(u):
+            return 0 <= u < UNITS
 
-        def tile_finished_by(u):
-            return u // 2 if 0 <= u < UNITS and u % 2 == 1 else None
+        def tile_at(s, first):
+            m, rest = divmod(s - first, 2)
+            return m if rest == 0 and 0 <= m <= LAST_TILE else None
 
-        for h in range(HEADS):
-            transpose_kq_head(0, h, nc.scalar.copy if h % 2 == 0 else nc.vector.tensor_copy)
-        kq_raw[1] = load_kq(1)
-        v_raw[1] = load_v(1)
-        score_matmuls(0, range(SCORE_BANKS))
+        transpose_q(0, 0)
+        copy_q(0, 0, nc.vector.tensor_copy)
+        transpose_k(0, 0)
+        copy_k(0, 0, nc.scalar.copy)
+        transpose_k(0, 1)
+        copy_k(0, 1, nc.vector.tensor_copy)
+        score_matmuls(0, 0)
+        transpose_k(0, 2)
+        copy_k(0, 2, nc.scalar.copy)
+        score_matmuls(0, 1)
+        transpose_k(0, 3)
+        copy_k(0, 3, nc.vector.tensor_copy)
+        score_matmuls(0, 2)
+        score_matmuls(0, 3)
         seed_maximum(0)
+        load_k(1, 1)
+        load_q(1, 0, PACK)
 
-        half_frame = UNITS_PER_FRAME // 2
-        for s in range(UNITS + 7):
-            if s == half_frame - 1:
-                quantise_w()
-            if s == half_frame:
+        turn_kq = {
+            0: (("q", 0, 1),),
+            1: (("k", 1, 0),),
+            2: (("q", 0, 2),),
+            3: (("k", 1, 1),),
+            4: (("q", 0, 3),),
+            5: (("k", 1, 2),),
+            6: (("k", 1, 3), ("q", 1, 0)),
+            7: (("q", 1, 1),),
+            9: (("q", 1, 2),),
+            11: (("q", 1, 3),),
+        }
+        turn_w = {0: (0, 1), 1: (2, 3), 2: (4, 5), 3: (6,), 4: (7,)}
+
+        for s in range(UNITS + 8):
+            m_log = tile_at(s, 3)
+            m_turn = tile_at(s, 4)
+            m_recip = tile_at(s, 5)
+            m_attn = tile_at(s, 7)
+            m_o = tile_at(s, 8)
+            m_y = tile_at(s, 9)
+
+            for i in turn_w.get(s - 1, ()):
+                copy_w(i, nc.scalar.copy)
+            if m_o is not None:
+                round_o(m_o, 0, nc.scalar.copy)
+                round_o(m_o, 1, nc.vector.tensor_copy if m_o == LAST_TILE else nc.scalar.copy)
+            if m_log is not None:
+                log_of_sums(m_log)
+
+            if unit(s):
+                maximum_step(s, 1)
+                maximum_step(s, 2)
+                maximum_step(s, 3)
+            for kind, b, x in turn_kq.get(s - 1, ()):
+                (copy_k if kind == "k" else copy_q)(b, x, nc.vector.tensor_copy)
+            if m_recip is not None:
+                copy_reciprocals(m_recip, nc.vector.tensor_copy)
+            if m_attn is not None:
+                quantise_attn(m_attn)
+            if s == 2:
                 quantise_v(0)
-            if s == UNITS_PER_FRAME:
+            if s == 6:
+                for g in range(PASSES):
+                    quantise_w(g)
+            if s == 8:
                 quantise_v(1)
+            if unit(s):
+                maximum_end(s)
+            if m_y is not None:
+                store(m_y, 0, nc.vector.tensor_copy)
+                store(m_y, 1, nc.scalar.copy if m_y == LAST_TILE else nc.vector.tensor_copy)
+            for bank in range(SCORE_BANKS):
+                if unit(s):
+                    shift_bank(s, bank)
+                if unit(s + 1):
+                    score_matmuls(s + 1, bank)
+                if bank == 0 and unit(s + 1):
+                    seed_maximum(s + 1)
+            if m_o is not None:
+                quantise_o(m_o)
 
-            if tile_finished_by(s - 2) is not None:
-                log_of_sums(tile_finished_by(s - 2))
-                reciprocal_of_sums(tile_finished_by(s - 2))
-            if tile_finished_by(s - 7) is not None:
-                store(tile_finished_by(s - 7), 1)
-            if tile_finished_by(s - 5) is not None:
-                round_o(tile_finished_by(s - 5))
-            if s < UNITS_PER_FRAME:
-                b_side, first = divmod(2 * s, HEADS)
-                if first == 0:
-                    v_grouped[b_side] = single.tile([P, HEADS, HEAD_DIM, PACK], BF16, name="v_grouped", align_bytes=64)
-                for x in (first, first + 1):
-                    group_v_head(b_side, x)
-                if s % 2 == 0:
-                    for x in range(first, first + 4):
-                        if b_side == 0:
-                            transpose_w_rows(x)
-                        else:
-                            transpose_kq_head(1, x, nc.scalar.copy)
+            for kind, b, x in turn_kq.get(s, ()):
+                (transpose_k if kind == "k" else transpose_q)(b, x)
+            for i in turn_w.get(s, ()):
+                transpose_w(i)
+            if m_turn is not None:
+                turn_reciprocals(m_turn)
+            if unit(s - 1):
+                sum_over_heads(s - 1)
+            if m_attn is not None:
+                attention_times_v(m_attn)
+            if m_o is not None:
+                project(m_o)
 
-            maximum_and_normalise(unit_or_none(s), unit_or_none(s - 4))
-            if s < UNITS:
-                shift_by_maximum(s)
-            if tile_finished_by(s - 4) is not None:
-                quantise_attn(tile_finished_by(s - 4))
-            if tile_finished_by(s - 5) is not None:
-                quantise_o(tile_finished_by(s - 5))
-
-            if s + 1 < UNITS:
-                score_matmuls(s + 1, (0, 1))
-                seed_maximum(s + 1)
-            if tile_finished_by(s - 2) is not None:
-                reciprocal_to_psum(tile_finished_by(s - 2))
-            if s + 1 < UNITS:
-                score_matmuls(s + 1, (2, 3))
-            if tile_finished_by(s - 6) is not None:
-                store(tile_finished_by(s - 6), 0)
-            if tile_finished_by(s - 4) is not None:
-                attention_times_v(tile_finished_by(s - 4))
-            if tile_finished_by(s - 5) is not None:
-                project(tile_finished_by(s - 5))
-            if unit_or_none(s - 3) is not None:
-                normalise_on_gpsimd(s - 3)
-            if s < UNITS:
+            if m_log is not None:
+                reciprocal_of_sums(m_log)
+            if unit(s):
                 exponentials(s)
-                sum_over_heads(s)
+
+            if s == 0:
+                for h in range(HEADS):
+                    group_v_head(0, h)
+                load_v(1)
+            if s == 3:
+                for h in range(HEADS):
+                    group_v_head(1, h)
+            u = s - 5
+            if unit(u):
+                if u // 2 >= SHARED_TILES:
+                    normalise(u, nc.vector, 0, 4, recips_ps[u // 2])
+                    normalise(u, nc.gpsimd, 4, HEADS, recips[u // 2])
+                else:
+                    normalise(u, nc.gpsimd, 0, HEADS, recips[u // 2])

@@ -37,7 +37,10 @@ FLOPS = 2 * FRAMES * HEADS * TOKENS * TOKENS * HEAD_DIM * 2 + 2 * FRAMES * TOKEN
 
 SUM_BLOCKS = UNIT_COLS // P
 LAST_TILE = UNITS // 2 - 1
-SHARED_TILES = LAST_TILE - 1
+TAIL_RECIP = 5
+GPSIMD_SHIFTS = 6
+LOGS = {3: (0,), 7: (1, 2), 11: (3, 4), 13: (5,), 15: (6,)}
+TAIL_TILE = 3
 
 
 def tile_attention2_pa_kernel(tc, q, k, v, w_proj, out):
@@ -52,8 +55,8 @@ def tile_attention2_pa_kernel(tc, q, k, v, w_proj, out):
         double = stack.enter_context(tc.tile_pool(name="double", bufs=2))
         deep = stack.enter_context(tc.tile_pool(name="deep", bufs=7))
         score_psum = stack.enter_context(tc.psum_pool(name="score_psum", bufs=1))
-        sum_psum = stack.enter_context(tc.psum_pool(name="sum_psum", bufs=1))
-        aux_psum = stack.enter_context(tc.psum_pool(name="aux_psum", bufs=3))
+        sum_psum = stack.enter_context(tc.psum_pool(name="sum_psum", bufs=2))
+        aux_psum = stack.enter_context(tc.psum_pool(name="aux_psum", bufs=2))
 
         def rows_by_four(src):
             return src.rearrange("h (p x) d -> p h x d", x=PACK)
@@ -86,12 +89,14 @@ def tile_attention2_pa_kernel(tc, q, k, v, w_proj, out):
                 in_=v[b].rearrange("h (p t) d -> p h (t d)", t=PACK),
             )
 
-        w_raw = raw.tile([P, C_OUT // P, CHANNELS], BF16)
+        w_raw = []
 
         def load_w():
             w_rows = w_proj.rearrange("(i p) c -> p i c", p=P)
             for i0 in (0, 4):
-                nc.sync.dma_start(out=w_raw[:, i0 : i0 + 4, :], in_=w_rows[:, i0 : i0 + 4, :])
+                w_half = double.tile([P, 4, CHANNELS], BF16, tag="w_attn", name="w_half", align_bytes=64)
+                nc.sync.dma_start(out=w_half[:], in_=w_rows[:, i0 : i0 + 4, :])
+                w_raw.append(w_half)
 
         load_q(0, 0, 1)
         load_k(0, 4)
@@ -159,9 +164,12 @@ def tile_attention2_pa_kernel(tc, q, k, v, w_proj, out):
             )
 
         def transpose_w(i):
-            ps = aux_psum.tile([P, PASSES * PACK, P], BF16, tag="aux", name="w_ps")
+            if i % 2 == 0:
+                ps = aux_psum.tile([P, PASSES * PACK, P], BF16, tag="aux", name="w_ps")
+            else:
+                ps = sum_psum.tile([P, PASSES * PACK, P], BF16, tag="sum", name="w_ps")
             for c in range(PASSES * PACK):
-                nc.tensor.transpose(ps[:, c, :], w_raw[:, i, c * P : (c + 1) * P], identity[:])
+                nc.tensor.transpose(ps[:, c, :], w_raw[i // 4][:, i % 4, c * P : (c + 1) * P], identity[:])
             turned["w", i] = ps
 
         def copy_w(i, copy):
@@ -178,6 +186,7 @@ def tile_attention2_pa_kernel(tc, q, k, v, w_proj, out):
             )
 
         scores = {}
+        seeds = {}
         running = {}
         tops = {}
         expd = {}
@@ -209,14 +218,19 @@ def tile_attention2_pa_kernel(tc, q, k, v, w_proj, out):
             return s_ps[:].rearrange("p i t n -> p i n t")
 
         def seed_maximum(u):
-            running[u] = double.tile([P, HEADS_PER_BANK, CHUNK, PACK], F32, name="run")
-            nc.scalar.copy(out=running[u][:], in_=bank_view(scores[u][0]))
+            seeds[u] = double.tile([P, HEADS_PER_BANK, CHUNK, PACK], F32, name="seed")
+            nc.scalar.copy(out=seeds[u][:], in_=bank_view(scores[u][0]))
 
         def maximum_step(u, bank):
-            run = running[u]
+            if bank == 1:
+                running[u] = double.tile([P, HEADS_PER_BANK, CHUNK, PACK], F32, name="run")
+            so_far = seeds[u] if bank == 1 else running[u]
             for i in range(HEADS_PER_BANK):
                 nc.vector.tensor_tensor(
-                    out=run[:, i], in0=scores[u][bank][:, i].rearrange("p t n -> p n t"), in1=run[:, i], op=ALU.max
+                    out=running[u][:, i],
+                    in0=scores[u][bank][:, i].rearrange("p t n -> p n t"),
+                    in1=so_far[:, i],
+                    op=ALU.max,
                 )
 
         def maximum_end(u):
@@ -227,9 +241,11 @@ def tile_attention2_pa_kernel(tc, q, k, v, w_proj, out):
             if bank == 0:
                 expd[u] = deep.tile([P, HEADS, UNIT_COLS], F32, name="e")
             h0 = bank * HEADS_PER_BANK
-            nc.vector.tensor_tensor(
+            on_gpsimd = bank == 0 and u < GPSIMD_SHIFTS
+            engine = nc.gpsimd if on_gpsimd else nc.vector
+            engine.tensor_tensor(
                 out=expd[u][:, h0 : h0 + HEADS_PER_BANK, :].rearrange("p i (n t) -> p i n t", t=PACK),
-                in0=bank_view(scores[u][bank]),
+                in0=seeds[u][:] if on_gpsimd else bank_view(scores[u][bank]),
                 in1=tops[u][:].unsqueeze(1).to_broadcast([P, HEADS_PER_BANK, CHUNK, PACK]),
                 op=ALU.subtract,
             )
@@ -240,7 +256,7 @@ def tile_attention2_pa_kernel(tc, q, k, v, w_proj, out):
         def sum_over_heads(u):
             m, half = u // 2, u % 2
             if half == 0:
-                totals[m] = sum_psum.tile([P, 2 * SUM_BLOCKS, P], F32, name="total")
+                totals[m] = sum_psum.tile([P, 2 * SUM_BLOCKS, P], F32, tag="sum", name="total")
             for i in range(SUM_BLOCKS):
                 for h in range(HEADS):
                     nc.tensor.matmul(
@@ -252,7 +268,6 @@ def tile_attention2_pa_kernel(tc, q, k, v, w_proj, out):
                         is_transpose=True,
                     )
 
-        logs = {}
         recips_t = {}
         recips_ps = {}
         recips = {}
@@ -264,35 +279,40 @@ def tile_attention2_pa_kernel(tc, q, k, v, w_proj, out):
         y_banks = {}
 
         def log_of_sums(m):
-            logs[m] = double.tile([P, TILE_COLS], F32, name="log_total")
-            nc.scalar.activation(out=logs[m][:], in_=totals[m][:].rearrange("c i p -> c (i p)"), func=ACT.Ln)
+            recips_t[m] = double.tile([P, TILE_COLS], F32, name="recip_t")
+            nc.scalar.activation(out=recips_t[m][:], in_=totals[m][:].rearrange("c i p -> c (i p)"), func=ACT.Ln)
 
         def reciprocal_of_sums(m):
-            recips_t[m] = double.tile([P, TILE_COLS], F32, name="recip_t")
-            nc.scalar.activation(out=recips_t[m][:], in_=logs[m][:], func=ACT.Exp, scale=-1.0)
+            nc.scalar.activation(out=recips_t[m][:], in_=recips_t[m][:], func=ACT.Exp, scale=-1.0)
 
         def turn_reciprocals(m):
-            if m < SHARED_TILES:
+            if m < TAIL_RECIP:
                 recips_ps[m] = aux_psum.tile([P, TILE_COLS], F32, tag="aux", name="recip_ps")
             else:
-                recips_ps[m] = score_psum.tile([P, TILE_COLS], F32, name="s_ps%d" % (m - SHARED_TILES))
+                recips_ps[m] = score_psum.tile([P, TILE_COLS], F32, name="s_ps%d" % (m % 2))
             for i in range(TILE_COLS // P):
                 cols = slice(i * P, (i + 1) * P)
                 nc.tensor.transpose(recips_ps[m][:, cols], recips_t[m][:, cols], identity_f32[:])
 
-        def copy_reciprocals(m, copy):
-            recips[m] = double.tile([P, TILE_COLS], F32, name="recip")
-            copy(out=recips[m][:], in_=recips_ps[m][:])
+        def copy_reciprocals(m):
+            both = double.tile([P, TILE_COLS], F32, name="recip_both")
+            nc.vector.tensor_copy(out=both[:], in_=recips_ps[m][:])
+            recips[2 * m] = both[:, :UNIT_COLS]
+            recips[2 * m + 1] = both[:, UNIT_COLS:]
+
+        def hand_over_reciprocals(u):
+            copy = double.tile([P, UNIT_COLS], F32, name="recip_odd")
+            nc.vector.tensor_copy(out=copy[:], in_=recips[u])
+            recips[u] = copy[:]
 
         def normalise(u, engine, h0, h1, factors):
             m, half = u // 2, u % 2
             if m not in attn:
-                attn[m] = double.tile([P, HEADS, TILE_COLS], BF16, name="attn", align_bytes=64)
-            cols = slice(half * UNIT_COLS, (half + 1) * UNIT_COLS)
+                attn[m] = double.tile([P, HEADS, TILE_COLS], BF16, tag="w_attn", name="attn", align_bytes=64)
             engine.tensor_tensor(
-                out=attn[m][:, h0:h1, cols],
+                out=attn[m][:, h0:h1, half * UNIT_COLS : (half + 1) * UNIT_COLS],
                 in0=expd[u][:, h0:h1, :],
-                in1=factors[:, cols].unsqueeze(1).to_broadcast([P, h1 - h0, UNIT_COLS]),
+                in1=factors.unsqueeze(1).to_broadcast([P, h1 - h0, UNIT_COLS]),
                 op=ALU.mult,
             )
 
@@ -311,7 +331,7 @@ def tile_attention2_pa_kernel(tc, q, k, v, w_proj, out):
             a_codes, a_scales = a_words[m]
             o_banks[m] = []
             for g in range(PASSES):
-                o_ps = aux_psum.tile([P, PACK, TILE_Q], F32, tag="aux")
+                o_ps = aux_psum.tile([P, PACK, TILE_Q], F32, tag="aux", name="o_ps")
                 for t in range(PACK):
                     h = g * PACK + t
                     cols = slice(h * TILE_Q, (h + 1) * TILE_Q)
@@ -345,7 +365,10 @@ def tile_attention2_pa_kernel(tc, q, k, v, w_proj, out):
             o_codes, o_scales = o_words[m]
             y_banks[m] = []
             for c0 in range(0, C_OUT, BANK):
-                y_ps = aux_psum.tile([P, BANK], F32, tag="aux")
+                if m < TAIL_TILE:
+                    y_ps = aux_psum.tile([P, BANK], F32, tag="aux", name="y_ps")
+                else:
+                    y_ps = score_psum.tile([P, BANK], F32, name="s_ps%d" % (2 + c0 // BANK))
                 for g in range(PASSES):
                     o_cols = slice(g * TILE_Q, (g + 1) * TILE_Q)
                     w_cols = slice(g * C_OUT + c0, g * C_OUT + c0 + BANK)
@@ -390,100 +413,165 @@ def tile_attention2_pa_kernel(tc, q, k, v, w_proj, out):
         score_matmuls(0, 2)
         score_matmuls(0, 3)
         seed_maximum(0)
+        transpose_q(0, 1)
+        copy_q(0, 1, nc.scalar.copy)
+        score_matmuls(1, 0)
         load_k(1, 1)
         load_q(1, 0, PACK)
 
         turn_kq = {
-            0: (("q", 0, 1),),
-            1: (("k", 1, 0),),
-            2: (("q", 0, 2),),
-            3: (("k", 1, 1),),
-            4: (("q", 0, 3),),
-            5: (("k", 1, 2),),
-            6: (("k", 1, 3), ("q", 1, 0)),
-            7: (("q", 1, 1),),
-            9: (("q", 1, 2),),
-            11: (("q", 1, 3),),
+            1: (("q", 0, 2),),
+            2: (("k", 1, 0),),
+            3: (("q", 0, 3),),
+            4: (("k", 1, 1), ("k", 1, 2)),
+            5: (("k", 1, 3), ("q", 1, 0)),
+            6: (("q", 1, 1), ("q", 1, 2)),
         }
-        turn_w = {0: (0, 1), 1: (2, 3), 2: (4, 5), 3: (6,), 4: (7,)}
+        turn_w = {0: (0, 1), 1: (2, 3), 2: (4, 5), 3: (6, 7)}
 
-        for s in range(UNITS + 8):
-            m_log = tile_at(s, 3)
-            m_turn = tile_at(s, 4)
-            m_recip = tile_at(s, 5)
-            m_attn = tile_at(s, 7)
-            m_o = tile_at(s, 8)
-            m_y = tile_at(s, 9)
+        half = HEADS // 2
+        for s in range(UNITS):
+            m_turn = tile_at(s, 6)
+            m_attn = tile_at(s, 8)
+            m_av = tile_at(s, 9)
+            m_o = tile_at(s, 10)
+            m_y = tile_at(s, 11)
+            logs_now = LOGS.get(s, ())
+            exps_now = LOGS.get(s - 1, ())
 
+            for kind, b, x in turn_kq.get(s - 1, ()):
+                (copy_k if kind == "k" else copy_q)(b, x, nc.scalar.copy)
+            if m_o is not None:
+                for g in range(PASSES):
+                    round_o(m_o, g, nc.scalar.copy)
+            for m in exps_now[:1]:
+                reciprocal_of_sums(m)
+            if m_turn is not None:
+                turn_reciprocals(m_turn)
+            if s < GPSIMD_SHIFTS:
+                seed_maximum(s + 1)
+            if unit(s - 1):
+                exponentials(s - 1)
             for i in turn_w.get(s - 1, ()):
                 copy_w(i, nc.scalar.copy)
-            if m_o is not None:
-                round_o(m_o, 0, nc.scalar.copy)
-                round_o(m_o, 1, nc.vector.tensor_copy if m_o == LAST_TILE else nc.scalar.copy)
-            if m_log is not None:
-                log_of_sums(m_log)
+            if m_y is not None:
+                store(m_y, 0, nc.scalar.copy)
+                store(m_y, 1, nc.scalar.copy)
+            for m in logs_now:
+                log_of_sums(m)
 
-            if unit(s):
-                maximum_step(s, 1)
-                maximum_step(s, 2)
-                maximum_step(s, 3)
-            for kind, b, x in turn_kq.get(s - 1, ()):
-                (copy_k if kind == "k" else copy_q)(b, x, nc.vector.tensor_copy)
-            if m_recip is not None:
-                copy_reciprocals(m_recip, nc.vector.tensor_copy)
-            if m_attn is not None:
-                quantise_attn(m_attn)
+            for bank in range(1, SCORE_BANKS):
+                maximum_step(s, bank)
             if s == 2:
                 quantise_v(0)
-            if s == 6:
+            if s == 7:
                 for g in range(PASSES):
                     quantise_w(g)
-            if s == 8:
+            if s == 5:
                 quantise_v(1)
-            if unit(s):
-                maximum_end(s)
-            if m_y is not None:
-                store(m_y, 0, nc.vector.tensor_copy)
-                store(m_y, 1, nc.scalar.copy if m_y == LAST_TILE else nc.vector.tensor_copy)
-            for bank in range(SCORE_BANKS):
-                if unit(s):
-                    shift_bank(s, bank)
-                if unit(s + 1):
-                    score_matmuls(s + 1, bank)
-                if bank == 0 and unit(s + 1):
-                    seed_maximum(s + 1)
             if m_o is not None:
                 quantise_o(m_o)
+            if m_attn is not None:
+                quantise_attn(m_attn)
+            maximum_end(s)
+            if m_turn is not None:
+                copy_reciprocals(m_turn)
+            elif unit(s - 6):
+                hand_over_reciprocals(s - 6)
+            for bank in range(SCORE_BANKS):
+                shift_bank(s, bank)
+                if unit(s + 1) and (bank or s >= GPSIMD_SHIFTS):
+                    score_matmuls(s + 1, bank)
+                    if bank == 0:
+                        seed_maximum(s + 1)
+                if s == 7 and bank == 1:
+                    transpose_q(1, 3)
+            if s + 1 < GPSIMD_SHIFTS:
+                score_matmuls(s + 2, 0)
+            if s == 7:
+                copy_q(1, 3, nc.vector.tensor_copy)
+
+            for m in exps_now[1:]:
+                reciprocal_of_sums(m)
 
             for kind, b, x in turn_kq.get(s, ()):
                 (transpose_k if kind == "k" else transpose_q)(b, x)
             for i in turn_w.get(s, ()):
                 transpose_w(i)
-            if m_turn is not None:
-                turn_reciprocals(m_turn)
-            if unit(s - 1):
-                sum_over_heads(s - 1)
-            if m_attn is not None:
-                attention_times_v(m_attn)
             if m_o is not None:
                 project(m_o)
+            if m_av is not None:
+                attention_times_v(m_av)
+            if unit(s - 1):
+                sum_over_heads(s - 1)
 
-            if m_log is not None:
-                reciprocal_of_sums(m_log)
-            if unit(s):
-                exponentials(s)
-
-            if s == 0:
-                for h in range(HEADS):
-                    group_v_head(0, h)
+            if s < 2 * FRAMES:
+                for h in range(s % 2 * half, s % 2 * half + half):
+                    group_v_head(s // 2, h)
+            if s == 1:
                 load_v(1)
-            if s == 3:
-                for h in range(HEADS):
-                    group_v_head(1, h)
-            u = s - 5
-            if unit(u):
-                if u // 2 >= SHARED_TILES:
-                    normalise(u, nc.vector, 0, 4, recips_ps[u // 2])
-                    normalise(u, nc.gpsimd, 4, HEADS, recips[u // 2])
-                else:
-                    normalise(u, nc.gpsimd, 0, HEADS, recips[u // 2])
+            if unit(s - 6):
+                normalise(s - 6, nc.gpsimd, 0, HEADS, recips[s - 6])
+
+        vec, sca = nc.vector.tensor_copy, nc.scalar.copy
+
+        def factors(u):
+            return recips_ps[u // 2][:, u % 2 * UNIT_COLS : (u % 2 + 1) * UNIT_COLS]
+
+        exponentials(15)
+        reciprocal_of_sums(6)
+        turn_reciprocals(5)
+        sum_over_heads(15)
+        log_of_sums(7)
+        reciprocal_of_sums(7)
+        for g in range(PASSES):
+            round_o(3, g, vec)
+        quantise_o(3)
+        project(3)
+        quantise_attn(4)
+        attention_times_v(4)
+        turn_reciprocals(6)
+        copy_reciprocals(5)
+        normalise(10, nc.gpsimd, 0, HEADS, recips[10])
+        normalise(11, nc.vector, 0, HEADS, factors(11))
+        copy_reciprocals(6)
+        normalise(12, nc.vector, 0, HEADS, factors(12))
+        for g in range(PASSES):
+            round_o(4, g, vec)
+        store(3, 0, sca)
+        store(3, 1, sca)
+        quantise_attn(5)
+        normalise(13, nc.gpsimd, 0, half, recips[13])
+        attention_times_v(5)
+        quantise_o(4)
+        project(4)
+        turn_reciprocals(7)
+        normalise(13, nc.vector, half, HEADS, factors(13))
+        for g in range(PASSES):
+            round_o(5, g, sca)
+        quantise_attn(6)
+        attention_times_v(6)
+        copy_reciprocals(7)
+        normalise(14, nc.gpsimd, 0, half, recips[14])
+        normalise(15, nc.vector, 0, HEADS, factors(15))
+        normalise(14, nc.vector, half, HEADS, factors(14))
+        store(4, 0, sca)
+        store(4, 1, sca)
+        quantise_o(5)
+        project(5)
+        for g in range(PASSES):
+            round_o(6, g, sca)
+        store(5, 0, sca)
+        store(5, 1, sca)
+        quantise_o(6)
+        project(6)
+        quantise_attn(7)
+        attention_times_v(7)
+        store(6, 0, sca)
+        store(6, 1, vec)
+        round_o(7, 0, vec)
+        round_o(7, 1, sca)
+        quantise_o(7)
+        project(7)
+        store(7, 0, sca)
+        store(7, 1, vec)

@@ -439,8 +439,10 @@ def tile_attention2_pa_kernel(tc, q, k, v, w_proj, out):
             logs_now = LOGS.get(s, ())
             exps_now = LOGS.get(s - 1, ())
 
-            for kind, b, x in turn_kq.get(s - 1, ()):
-                (copy_k if kind == "k" else copy_q)(b, x, nc.scalar.copy)
+            kq_on_vector = s in (3,)
+            if not kq_on_vector:
+                for kind, b, x in turn_kq.get(s - 1, ()):
+                    (copy_k if kind == "k" else copy_q)(b, x, nc.scalar.copy)
             if m_o is not None:
                 for g in range(PASSES):
                     round_o(m_o, g, nc.scalar.copy)
@@ -455,13 +457,17 @@ def tile_attention2_pa_kernel(tc, q, k, v, w_proj, out):
             for i in turn_w.get(s - 1, ()):
                 copy_w(i, nc.scalar.copy)
             if m_y is not None:
-                store(m_y, 0, nc.scalar.copy)
                 store(m_y, 1, nc.scalar.copy)
             for m in logs_now:
                 log_of_sums(m)
 
             for bank in range(1, SCORE_BANKS):
                 maximum_step(s, bank)
+            if kq_on_vector:
+                for kind, b, x in turn_kq.get(s - 1, ()):
+                    (copy_k if kind == "k" else copy_q)(b, x, nc.vector.tensor_copy)
+            if m_y is not None:
+                store(m_y, 0, nc.vector.tensor_copy)
             if s == 2:
                 quantise_v(0)
             if s == 7:
@@ -518,60 +524,58 @@ def tile_attention2_pa_kernel(tc, q, k, v, w_proj, out):
         def factors(u):
             return recips_ps[u // 2][:, u % 2 * UNIT_COLS : (u % 2 + 1) * UNIT_COLS]
 
+        turn_reciprocals(5)
         exponentials(15)
         reciprocal_of_sums(6)
-        turn_reciprocals(5)
+        turn_reciprocals(6)
         sum_over_heads(15)
         log_of_sums(7)
         reciprocal_of_sums(7)
-        for g in range(PASSES):
-            round_o(3, g, vec)
-        quantise_o(3)
-        project(3)
+        normalise(11, nc.vector, 0, HEADS, factors(11))
         quantise_attn(4)
-        attention_times_v(4)
-        turn_reciprocals(6)
         copy_reciprocals(5)
         normalise(10, nc.gpsimd, 0, HEADS, recips[10])
-        normalise(11, nc.vector, 0, HEADS, factors(11))
-        copy_reciprocals(6)
+        for g in range(PASSES):
+            round_o(3, g, vec)
+        attention_times_v(4)
         normalise(12, nc.vector, 0, HEADS, factors(12))
-        for g in range(PASSES):
-            round_o(4, g, vec)
-        store(3, 0, sca)
-        store(3, 1, sca)
+        normalise(13, nc.vector, 0, HEADS, factors(13))
+        quantise_o(3)
         quantise_attn(5)
-        normalise(13, nc.gpsimd, 0, half, recips[13])
-        attention_times_v(5)
-        quantise_o(4)
-        project(4)
         turn_reciprocals(7)
-        normalise(13, nc.vector, half, HEADS, factors(13))
-        for g in range(PASSES):
-            round_o(5, g, sca)
-        quantise_attn(6)
-        attention_times_v(6)
         copy_reciprocals(7)
         normalise(14, nc.gpsimd, 0, half, recips[14])
+        project(3)
+        for g in range(PASSES):
+            round_o(4, g, sca)
+        attention_times_v(5)
         normalise(15, nc.vector, 0, HEADS, factors(15))
         normalise(14, nc.vector, half, HEADS, factors(14))
-        store(4, 0, sca)
-        store(4, 1, sca)
-        quantise_o(5)
-        project(5)
+        store(3, 0, sca)
+        store(3, 1, sca)
         for g in range(PASSES):
-            round_o(6, g, sca)
-        store(5, 0, sca)
-        store(5, 1, sca)
-        quantise_o(6)
-        project(6)
+            round_o(5, g, sca)
+        quantise_o(4)
+        project(4)
         quantise_attn(7)
         attention_times_v(7)
-        store(6, 0, sca)
-        store(6, 1, vec)
-        round_o(7, 0, vec)
-        round_o(7, 1, sca)
+        quantise_o(5)
+        quantise_attn(6)
+        round_o(7, 0, sca)
+        round_o(7, 1, vec)
+        attention_times_v(6)
+        store(4, 0, sca)
+        store(4, 1, vec)
         quantise_o(7)
+        project(5)
+        round_o(6, 0, sca)
+        round_o(6, 1, vec)
+        store(5, 0, sca)
+        store(5, 1, vec)
         project(7)
+        quantise_o(6)
         store(7, 0, sca)
         store(7, 1, vec)
+        project(6)
+        store(6, 0, sca)
+        store(6, 1, vec)

@@ -38,6 +38,7 @@ FLOPS = 2 * FRAMES * HEADS * TOKENS * TOKENS * HEAD_DIM * 2 + 2 * FRAMES * TOKEN
 SUM_BLOCKS = UNIT_COLS // P
 LAST_TILE = UNITS // 2 - 1
 TAIL_RECIP = 5
+W_ON_SUMS = (0, 1, 3, 6)
 GPSIMD_SHIFTS = 6
 LOGS = {3: (0,), 7: (1, 2), 11: (3, 4), 13: (5,), 15: (6,)}
 TAIL_TILE = 3
@@ -91,18 +92,17 @@ def tile_attention2_pa_kernel(tc, q, k, v, w_proj, out):
 
         w_raw = []
 
-        def load_w():
-            w_rows = w_proj.rearrange("(i p) c -> p i c", p=P)
-            for i0 in (0, 4):
-                w_half = double.tile([P, 4, CHANNELS], BF16, tag="w_attn", name="w_half", align_bytes=64)
-                nc.sync.dma_start(out=w_half[:], in_=w_rows[:, i0 : i0 + 4, :])
-                w_raw.append(w_half)
+        def load_w(i0):
+            w_half = double.tile([P, 4, CHANNELS], BF16, tag="w_attn", name="w_half", align_bytes=64)
+            nc.sync.dma_start(out=w_half[:], in_=w_proj.rearrange("(i p) c -> p i c", p=P)[:, i0 : i0 + 4, :])
+            w_raw.append(w_half)
 
         load_q(0, 0, 1)
         load_k(0, 4)
+        load_w(0)
         load_q(0, 1, PACK)
         load_v(0)
-        load_w()
+        load_w(4)
 
         identity = const.tile([P, P], BF16)
         make_identity(nc, identity[:])
@@ -126,7 +126,10 @@ def tile_attention2_pa_kernel(tc, q, k, v, w_proj, out):
         turned = {}
 
         def transpose_k(b, pair):
-            ps = aux_psum.tile([P, 2, PACK, P], BF16, tag="aux", name="k_ps")
+            if b == 0 and pair in (1, 2):
+                ps = sum_psum.tile([P, 2, PACK, P], BF16, tag="sum", name="k_ps")
+            else:
+                ps = aux_psum.tile([P, 2, PACK, P], BF16, tag="aux", name="k_ps")
             for i in range(2):
                 for t in range(PACK):
                     nc.tensor.transpose(ps[:, i, t, :], k_raw[b][:, 2 * pair + i, t, :], identity[:])
@@ -164,7 +167,7 @@ def tile_attention2_pa_kernel(tc, q, k, v, w_proj, out):
             )
 
         def transpose_w(i):
-            if i % 2 == 0:
+            if i not in W_ON_SUMS:
                 ps = aux_psum.tile([P, PASSES * PACK, P], BF16, tag="aux", name="w_ps")
             else:
                 ps = sum_psum.tile([P, PASSES * PACK, P], BF16, tag="sum", name="w_ps")
@@ -398,21 +401,24 @@ def tile_attention2_pa_kernel(tc, q, k, v, w_proj, out):
             m, rest = divmod(s - first, 2)
             return m if rest == 0 and 0 <= m <= LAST_TILE else None
 
+        idle_ps = score_psum.tile([P, P], F32, name="s_ps3")
+        for i in range(4):
+            nc.tensor.matmul(out=idle_ps[:], lhsT=identity_f32[:], rhs=identity_f32[:], start=True, stop=True)
         transpose_q(0, 0)
         copy_q(0, 0, nc.vector.tensor_copy)
         transpose_k(0, 0)
         copy_k(0, 0, nc.scalar.copy)
         transpose_k(0, 1)
         copy_k(0, 1, nc.vector.tensor_copy)
-        score_matmuls(0, 0)
         transpose_k(0, 2)
         copy_k(0, 2, nc.scalar.copy)
-        score_matmuls(0, 1)
+        score_matmuls(0, 0)
         transpose_k(0, 3)
         copy_k(0, 3, nc.vector.tensor_copy)
+        seed_maximum(0)
+        score_matmuls(0, 1)
         score_matmuls(0, 2)
         score_matmuls(0, 3)
-        seed_maximum(0)
         transpose_q(0, 1)
         copy_q(0, 1, nc.scalar.copy)
         score_matmuls(1, 0)
@@ -427,7 +433,7 @@ def tile_attention2_pa_kernel(tc, q, k, v, w_proj, out):
             5: (("k", 1, 3), ("q", 1, 0)),
             6: (("q", 1, 1), ("q", 1, 2)),
         }
-        turn_w = {0: (0, 1), 1: (2, 3), 2: (4, 5), 3: (6, 7)}
+        turn_w = {0: (3, 4), 1: (5,), 2: (6,), 3: (7,)}
 
         half = HEADS // 2
         for s in range(UNITS):
@@ -439,7 +445,7 @@ def tile_attention2_pa_kernel(tc, q, k, v, w_proj, out):
             logs_now = LOGS.get(s, ())
             exps_now = LOGS.get(s - 1, ())
 
-            kq_on_vector = s in (3,)
+            kq_on_vector = s in (2, 3, 4)
             if not kq_on_vector:
                 for kind, b, x in turn_kq.get(s - 1, ()):
                     (copy_k if kind == "k" else copy_q)(b, x, nc.scalar.copy)
@@ -450,10 +456,14 @@ def tile_attention2_pa_kernel(tc, q, k, v, w_proj, out):
                 reciprocal_of_sums(m)
             if m_turn is not None:
                 turn_reciprocals(m_turn)
-            if s < GPSIMD_SHIFTS:
-                seed_maximum(s + 1)
             if unit(s - 1):
                 exponentials(s - 1)
+            if s < GPSIMD_SHIFTS:
+                seed_maximum(s + 1)
+            if s == 0:
+                for i in range(3):
+                    transpose_w(i)
+                    copy_w(i, nc.scalar.copy)
             for i in turn_w.get(s - 1, ()):
                 copy_w(i, nc.scalar.copy)
             if m_y is not None:

@@ -54,6 +54,7 @@ def tile_attention2_pa_kernel(tc, q, k, v, w_proj, out):
         keep = stack.enter_context(tc.tile_pool(name="keep", bufs=1))
         single = stack.enter_context(tc.tile_pool(name="single", bufs=1))
         double = stack.enter_context(tc.tile_pool(name="double", bufs=2))
+        triple = stack.enter_context(tc.tile_pool(name="triple", bufs=3))
         deep = stack.enter_context(tc.tile_pool(name="deep", bufs=7))
         score_psum = stack.enter_context(tc.psum_pool(name="score_psum", bufs=1))
         sum_psum = stack.enter_context(tc.psum_pool(name="sum_psum", bufs=2))
@@ -320,8 +321,8 @@ def tile_attention2_pa_kernel(tc, q, k, v, w_proj, out):
             )
 
         def quantise_attn(m):
-            a_codes = double.tile([P, HEADS * TILE_Q], U32, align_bytes=64)
-            a_scales = double.tile([P, HEADS * TILE_Q], U8, align_bytes=64)
+            a_codes = triple.tile([P, HEADS * TILE_Q], U32, align_bytes=64)
+            a_scales = triple.tile([P, HEADS * TILE_Q], U8, align_bytes=64)
             nc.vector.quantize_mx(
                 out=a_codes[:].bitcast(FP8X4),
                 scales=a_scales[:],
@@ -351,12 +352,12 @@ def tile_attention2_pa_kernel(tc, q, k, v, w_proj, out):
 
         def round_o(m, g, copy):
             if g == 0:
-                o_grouped[m] = double.tile([P, PASSES, TILE_Q, PACK], BF16, name="o_grouped", align_bytes=64)
+                o_grouped[m] = triple.tile([P, PASSES, TILE_Q, PACK], BF16, name="o_grouped", align_bytes=64)
             copy(out=o_grouped[m][:, g, :, :], in_=o_banks[m][g][:].rearrange("p t n -> p n t"))
 
         def quantise_o(m):
-            o_codes = double.tile([P, PASSES * TILE_Q], U32, align_bytes=64)
-            o_scales = double.tile([P, PASSES * TILE_Q], U8, align_bytes=64)
+            o_codes = triple.tile([P, PASSES * TILE_Q], U32, align_bytes=64)
+            o_scales = triple.tile([P, PASSES * TILE_Q], U8, align_bytes=64)
             nc.vector.quantize_mx(
                 out=o_codes[:].bitcast(FP8X4),
                 scales=o_scales[:],
@@ -370,6 +371,8 @@ def tile_attention2_pa_kernel(tc, q, k, v, w_proj, out):
             for c0 in range(0, C_OUT, BANK):
                 if m < TAIL_TILE:
                     y_ps = aux_psum.tile([P, BANK], F32, tag="aux", name="y_ps")
+                elif m in (5, 7):
+                    y_ps = sum_psum.tile([P, BANK], F32, tag="sum", name="y_ps")
                 else:
                     y_ps = score_psum.tile([P, BANK], F32, name="s_ps%d" % (2 + c0 // BANK))
                 for g in range(PASSES):
@@ -535,57 +538,57 @@ def tile_attention2_pa_kernel(tc, q, k, v, w_proj, out):
             return recips_ps[u // 2][:, u % 2 * UNIT_COLS : (u % 2 + 1) * UNIT_COLS]
 
         turn_reciprocals(5)
-        exponentials(15)
         reciprocal_of_sums(6)
+        exponentials(15)
         turn_reciprocals(6)
         sum_over_heads(15)
         log_of_sums(7)
         reciprocal_of_sums(7)
-        normalise(11, nc.vector, 0, HEADS, factors(11))
+        normalise(11, nc.vector, 0, 8, factors(11))
         quantise_attn(4)
         copy_reciprocals(5)
-        normalise(10, nc.gpsimd, 0, HEADS, recips[10])
-        for g in range(PASSES):
-            round_o(3, g, vec)
-        attention_times_v(4)
-        normalise(12, nc.vector, 0, HEADS, factors(12))
-        normalise(13, nc.vector, 0, HEADS, factors(13))
-        quantise_o(3)
-        quantise_attn(5)
+        normalise(10, nc.gpsimd, 0, 8, recips[10])
+        normalise(12, nc.vector, 0, 8, factors(12))
+        normalise(13, nc.vector, 0, 8, factors(13))
         turn_reciprocals(7)
-        copy_reciprocals(7)
-        normalise(14, nc.gpsimd, 0, half, recips[14])
+        round_o(3, 0, sca)
+        round_o(3, 1, sca)
+        attention_times_v(4)
+        quantise_attn(5)
+        quantise_attn(6)
+        quantise_o(3)
         project(3)
-        for g in range(PASSES):
-            round_o(4, g, sca)
+        copy_reciprocals(7)
+        normalise(14, nc.gpsimd, 0, 4, recips[14])
+        round_o(4, 0, sca)
+        round_o(4, 1, sca)
         attention_times_v(5)
-        normalise(15, nc.vector, 0, HEADS, factors(15))
-        normalise(14, nc.vector, half, HEADS, factors(14))
+        normalise(15, nc.vector, 0, 8, factors(15))
+        normalise(14, nc.vector, 4, 8, factors(14))
+        round_o(5, 0, sca)
+        round_o(5, 1, sca)
+        attention_times_v(6)
         store(3, 0, sca)
         store(3, 1, sca)
-        for g in range(PASSES):
-            round_o(5, g, sca)
+        round_o(6, 0, sca)
+        round_o(6, 1, sca)
         quantise_o(4)
         project(4)
+        quantise_o(5)
         quantise_attn(7)
         attention_times_v(7)
-        quantise_o(5)
-        quantise_attn(6)
+        quantise_o(6)
+        project(5)
         round_o(7, 0, sca)
         round_o(7, 1, vec)
-        attention_times_v(6)
         store(4, 0, sca)
-        store(4, 1, vec)
         quantise_o(7)
-        project(5)
-        round_o(6, 0, sca)
-        round_o(6, 1, vec)
+        store(4, 1, vec)
+        project(6)
         store(5, 0, sca)
         store(5, 1, vec)
         project(7)
-        quantise_o(6)
-        store(7, 0, sca)
-        store(7, 1, vec)
-        project(6)
         store(6, 0, sca)
         store(6, 1, vec)
+        store(7, 0, sca)
+        store(7, 1, vec)

@@ -120,7 +120,7 @@ def tile_attention2_pa_kernel(tc, q, k, v, w_proj, out):
             qT[b] = keep.tile([P, PACK, HEADS, P], BF16, name="qT%d" % b)
             v_codes[b] = keep.tile([P, HEADS * HEAD_DIM], U32, name="v_codes%d" % b, align_bytes=64)
             v_scales[b] = keep.tile([P, HEADS * HEAD_DIM], U8, name="v_scales%d" % b, align_bytes=64)
-        w_grouped = keep.tile([P, PASSES, C_OUT, PACK], BF16, align_bytes=64)
+        w_grouped = single.tile([P, PASSES, C_OUT, PACK], BF16, tag="w_y", name="w_grouped", align_bytes=64)
         w_codes = keep.tile([P, PASSES * C_OUT], U32, align_bytes=64)
         w_scales = keep.tile([P, PASSES * C_OUT], U8, align_bytes=64)
 
@@ -281,6 +281,7 @@ def tile_attention2_pa_kernel(tc, q, k, v, w_proj, out):
         o_grouped = {}
         o_words = {}
         y_banks = {}
+        y_slots = {}
 
         def log_of_sums(m):
             recips_t[m] = double.tile([P, TILE_COLS], F32, name="recip_t")
@@ -391,10 +392,12 @@ def tile_attention2_pa_kernel(tc, q, k, v, w_proj, out):
 
         def store(m, i, copy):
             b, j = divmod(m, TILES_PER_FRAME)
-            y = double.tile([P, BANK], F32, name="y%d" % i)
-            copy(out=y[:], in_=y_banks[m][i][:])
+            if m == 0 and not y_slots:
+                y_slots[0] = single.tile([P, 2 * PACK, BANK], F32, tag="w_y", name="y_slots", align_bytes=64)
+            y = y_slots[0][:, (2 * m + i) % (2 * PACK), :]
+            copy(out=y, in_=y_banks[m][i][:])
             nc.sync.dma_start(
-                out=out[b].rearrange("(p j) c -> p j c", j=PACK)[:, j, i * BANK : (i + 1) * BANK], in_=y[:]
+                out=out[b].rearrange("(p j) c -> p j c", j=PACK)[:, j, i * BANK : (i + 1) * BANK], in_=y
             )
 
         def unit(u):
@@ -459,9 +462,11 @@ def tile_attention2_pa_kernel(tc, q, k, v, w_proj, out):
                 reciprocal_of_sums(m)
             if m_turn is not None:
                 turn_reciprocals(m_turn)
+            if exps_now and s < GPSIMD_SHIFTS:
+                seed_maximum(s + 1)
             if unit(s - 1):
                 exponentials(s - 1)
-            if s < GPSIMD_SHIFTS:
+            if s < GPSIMD_SHIFTS and not exps_now:
                 seed_maximum(s + 1)
             if s == 0:
                 for i in range(3):

@@ -100,8 +100,8 @@ def tile_attention2_pa_kernel(tc, q, k, v, w_proj, out):
 
         load_q(0, 0, 1)
         load_k(0, 4)
-        load_w(0)
         load_q(0, 1, PACK)
+        load_w(0)
         load_v(0)
         load_w(4)
 
@@ -321,21 +321,25 @@ def tile_attention2_pa_kernel(tc, q, k, v, w_proj, out):
                 op=ALU.mult,
             )
 
-        def quantise_attn(m):
-            a_codes = triple.tile([P, HEADS * TILE_Q], U32, align_bytes=64)
-            a_scales = triple.tile([P, HEADS * TILE_Q], U8, align_bytes=64)
+        def quantise_attn(m, g0=0, g1=PASSES):
+            if g0 == 0:
+                a_codes = triple.tile([P, HEADS * TILE_Q], U32, align_bytes=64)
+                a_scales = triple.tile([P, HEADS * TILE_Q], U8, align_bytes=64)
+                a_words[m] = (a_codes, a_scales)
+            a_codes, a_scales = a_words[m]
+            cols = slice(g0 * PACK * TILE_Q, g1 * PACK * TILE_Q)
             nc.vector.quantize_mx(
-                out=a_codes[:].bitcast(FP8X4),
-                scales=a_scales[:],
-                in_=attn[m][:].rearrange("p h c -> p (h c)"),
+                out=a_codes[:, cols].bitcast(FP8X4),
+                scales=a_scales[:, cols],
+                in_=attn[m][:, g0 * PACK : g1 * PACK, :].rearrange("p h c -> p (h c)"),
             )
-            a_words[m] = (a_codes, a_scales)
 
-        def attention_times_v(m):
+        def attention_times_v(m, groups=range(PASSES)):
             b = m // TILES_PER_FRAME
             a_codes, a_scales = a_words[m]
-            o_banks[m] = []
-            for g in range(PASSES):
+            if m not in o_banks:
+                o_banks[m] = []
+            for g in groups:
                 o_ps = aux_psum.tile([P, PACK, TILE_Q], F32, tag="aux", name="o_ps")
                 for t in range(PACK):
                     h = g * PACK + t
@@ -356,39 +360,49 @@ def tile_attention2_pa_kernel(tc, q, k, v, w_proj, out):
                 o_grouped[m] = triple.tile([P, PASSES, TILE_Q, PACK], BF16, name="o_grouped", align_bytes=64)
             copy(out=o_grouped[m][:, g, :, :], in_=o_banks[m][g][:].rearrange("p t n -> p n t"))
 
-        def quantise_o(m):
-            o_codes = triple.tile([P, PASSES * TILE_Q], U32, align_bytes=64)
-            o_scales = triple.tile([P, PASSES * TILE_Q], U8, align_bytes=64)
+        def quantise_o(m, g0=0, g1=PASSES):
+            if g0 == 0:
+                o_codes = triple.tile([P, PASSES * TILE_Q], U32, align_bytes=64)
+                o_scales = triple.tile([P, PASSES * TILE_Q], U8, align_bytes=64)
+                o_words[m] = (o_codes, o_scales)
+            o_codes, o_scales = o_words[m]
+            cols = slice(g0 * TILE_Q, g1 * TILE_Q)
             nc.vector.quantize_mx(
-                out=o_codes[:].bitcast(FP8X4),
-                scales=o_scales[:],
-                in_=o_grouped[m][:].rearrange("p g n t -> p (g n t)"),
+                out=o_codes[:, cols].bitcast(FP8X4),
+                scales=o_scales[:, cols],
+                in_=o_grouped[m][:, g0:g1].rearrange("p g n t -> p (g n t)"),
             )
-            o_words[m] = (o_codes, o_scales)
 
         def project(m):
-            o_codes, o_scales = o_words[m]
+            open_projection(m)
+            for i in range(C_OUT // BANK):
+                for g in range(PASSES):
+                    project_pass(m, i, g)
+
+        def open_projection(m):
             y_banks[m] = []
-            for c0 in range(0, C_OUT, BANK):
+            for i in range(C_OUT // BANK):
                 if m < TAIL_TILE:
                     y_ps = aux_psum.tile([P, BANK], F32, tag="aux", name="y_ps")
-                elif m in (5, 7):
+                elif m in (4, 6):
                     y_ps = sum_psum.tile([P, BANK], F32, tag="sum", name="y_ps")
                 else:
-                    y_ps = score_psum.tile([P, BANK], F32, name="s_ps%d" % (2 + c0 // BANK))
-                for g in range(PASSES):
-                    o_cols = slice(g * TILE_Q, (g + 1) * TILE_Q)
-                    w_cols = slice(g * C_OUT + c0, g * C_OUT + c0 + BANK)
-                    nc.tensor.matmul_mx(
-                        out=y_ps[:],
-                        lhsT=o_codes[:, o_cols].bitcast(FP8X4),
-                        lhsT_scale=o_scales[:, o_cols],
-                        rhs=w_codes[:, w_cols].bitcast(FP8X4),
-                        rhs_scale=w_scales[:, w_cols],
-                        start=(g == 0),
-                        stop=(g == PASSES - 1),
-                    )
+                    y_ps = score_psum.tile([P, BANK], F32, name="s_ps%d" % (i if m == LAST_TILE else 2 + i))
                 y_banks[m].append(y_ps)
+
+        def project_pass(m, i, g):
+            o_codes, o_scales = o_words[m]
+            o_cols = slice(g * TILE_Q, (g + 1) * TILE_Q)
+            w_cols = slice(g * C_OUT + i * BANK, g * C_OUT + (i + 1) * BANK)
+            nc.tensor.matmul_mx(
+                out=y_banks[m][i][:],
+                lhsT=o_codes[:, o_cols].bitcast(FP8X4),
+                lhsT_scale=o_scales[:, o_cols],
+                rhs=w_codes[:, w_cols].bitcast(FP8X4),
+                rhs_scale=w_scales[:, w_cols],
+                start=(g == 0),
+                stop=(g == PASSES - 1),
+            )
 
         def store(m, i, copy):
             b, j = divmod(m, TILES_PER_FRAME)
@@ -408,7 +422,7 @@ def tile_attention2_pa_kernel(tc, q, k, v, w_proj, out):
             return m if rest == 0 and 0 <= m <= LAST_TILE else None
 
         idle_ps = score_psum.tile([P, P], F32, name="s_ps3")
-        for i in range(4):
+        for i in range(6):
             nc.tensor.matmul(out=idle_ps[:], lhsT=identity_f32[:], rhs=identity_f32[:], start=True, stop=True)
         transpose_q(0, 0)
         copy_q(0, 0, nc.vector.tensor_copy)
@@ -438,6 +452,7 @@ def tile_attention2_pa_kernel(tc, q, k, v, w_proj, out):
             4: (("k", 1, 1), ("k", 1, 2)),
             5: (("k", 1, 3), ("q", 1, 0)),
             6: (("q", 1, 1), ("q", 1, 2)),
+            8: (("q", 1, 3),),
         }
         turn_w = {0: (3, 4), 1: (5,), 2: (6,), 3: (7,)}
 
@@ -451,6 +466,8 @@ def tile_attention2_pa_kernel(tc, q, k, v, w_proj, out):
             logs_now = LOGS.get(s, ())
             exps_now = LOGS.get(s - 1, ())
 
+            if s < GPSIMD_SHIFTS and (s >= 4):
+                seed_maximum(s + 1)
             kq_on_vector = s in (2, 3, 4)
             if not kq_on_vector:
                 for kind, b, x in turn_kq.get(s - 1, ()):
@@ -462,11 +479,9 @@ def tile_attention2_pa_kernel(tc, q, k, v, w_proj, out):
                 reciprocal_of_sums(m)
             if m_turn is not None:
                 turn_reciprocals(m_turn)
-            if exps_now and s < GPSIMD_SHIFTS:
-                seed_maximum(s + 1)
             if unit(s - 1):
                 exponentials(s - 1)
-            if s < GPSIMD_SHIFTS and not exps_now:
+            if s < GPSIMD_SHIFTS and not (s >= 4):
                 seed_maximum(s + 1)
             if s == 0:
                 for i in range(3):
@@ -508,12 +523,8 @@ def tile_attention2_pa_kernel(tc, q, k, v, w_proj, out):
                     score_matmuls(s + 1, bank)
                     if bank == 0:
                         seed_maximum(s + 1)
-                if s == 7 and bank == 1:
-                    transpose_q(1, 3)
             if s + 1 < GPSIMD_SHIFTS:
                 score_matmuls(s + 2, 0)
-            if s == 7:
-                copy_q(1, 3, nc.vector.tensor_copy)
 
             for m in exps_now[1:]:
                 reciprocal_of_sums(m)
@@ -563,36 +574,44 @@ def tile_attention2_pa_kernel(tc, q, k, v, w_proj, out):
         quantise_attn(6)
         quantise_o(3)
         project(3)
-        copy_reciprocals(7)
-        normalise(14, nc.gpsimd, 0, 4, recips[14])
+        normalise(15, nc.vector, 0, 4, factors(15))
         round_o(4, 0, sca)
         round_o(4, 1, sca)
         attention_times_v(5)
-        normalise(15, nc.vector, 0, 8, factors(15))
-        normalise(14, nc.vector, 4, 8, factors(14))
+        quantise_o(4)
+        project(4)
+        copy_reciprocals(7)
+        normalise(14, nc.gpsimd, 4, 8, recips[14])
+        normalise(14, nc.vector, 0, 4, factors(14))
+        normalise(15, nc.vector, 4, 8, factors(15))
+        store(3, 0, sca)
+        store(3, 1, sca)
         round_o(5, 0, sca)
         round_o(5, 1, sca)
         attention_times_v(6)
-        store(3, 0, sca)
-        store(3, 1, sca)
+        store(4, 0, sca)
+        store(4, 1, sca)
         round_o(6, 0, sca)
         round_o(6, 1, sca)
-        quantise_o(4)
-        project(4)
         quantise_o(5)
-        quantise_attn(7)
-        attention_times_v(7)
-        quantise_o(6)
         project(5)
+        quantise_attn(7, 0, 1)
+        attention_times_v(7, (0,))
+        quantise_attn(7, 1, 2)
+        quantise_o(6)
+        attention_times_v(7, (1,))
+        project(6)
         round_o(7, 0, sca)
         round_o(7, 1, vec)
-        store(4, 0, sca)
-        quantise_o(7)
-        store(4, 1, vec)
-        project(6)
         store(5, 0, sca)
         store(5, 1, vec)
-        project(7)
+        quantise_o(7, 0, 1)
+        open_projection(7)
+        for i in range(C_OUT // BANK):
+            project_pass(7, i, 0)
+        quantise_o(7, 1, 2)
+        for i in range(C_OUT // BANK):
+            project_pass(7, i, 1)
         store(6, 0, sca)
         store(6, 1, vec)
         store(7, 0, sca)

@@ -105,10 +105,10 @@ def tile_attention2_pa_kernel(tc, q, k, v, w_proj, out):
         load_v(0)
         load_w(4)
 
-        identity = const.tile([P, P], BF16)
-        make_identity(nc, identity[:])
         identity_f32 = const.tile([P, P], F32)
         make_identity(nc, identity_f32[:])
+        identity = const.tile([P, P], BF16)
+        make_identity(nc, identity[:])
 
         kT = {}
         qT = {}
@@ -451,8 +451,8 @@ def tile_attention2_pa_kernel(tc, q, k, v, w_proj, out):
             3: (("q", 0, 3),),
             4: (("k", 1, 1), ("k", 1, 2)),
             5: (("k", 1, 3), ("q", 1, 0)),
-            6: (("q", 1, 1), ("q", 1, 2)),
-            8: (("q", 1, 3),),
+            6: (("q", 1, 1),),
+            8: (("q", 1, 2), ("q", 1, 3)),
         }
         turn_w = {0: (3, 4), 1: (5,), 2: (6,), 3: (7,)}
 

@@ -55,6 +55,8 @@ def tile_attention2_pa_kernel(tc, q, k, v, w_proj, out):
         single = stack.enter_context(tc.tile_pool(name="single", bufs=1))
         double = stack.enter_context(tc.tile_pool(name="double", bufs=2))
         triple = stack.enter_context(tc.tile_pool(name="triple", bufs=3))
+        fourfold = stack.enter_context(tc.tile_pool(name="fourfold", bufs=4))
+        fourfold = stack.enter_context(tc.tile_pool(name="fourfold", bufs=4))
         deep = stack.enter_context(tc.tile_pool(name="deep", bufs=7))
         score_psum = stack.enter_context(tc.psum_pool(name="score_psum", bufs=1))
         sum_psum = stack.enter_context(tc.psum_pool(name="sum_psum", bufs=2))
@@ -182,6 +184,22 @@ def tile_attention2_pa_kernel(tc, q, k, v, w_proj, out):
                 in_=turned["w", i][:].rearrange("p (g t) r -> p g r t", t=PACK),
             )
 
+        w_flat = {}
+
+        def copy_w_flat(i):
+            w_flat[i] = fourfold.tile([P, PASSES * PACK, P], BF16, name="w_flat")
+            nc.scalar.copy(out=w_flat[i][:], in_=turned["w", i][:])
+
+        def group_w(i):
+            nc.gpsimd.tensor_scalar(
+                out=w_grouped[:, :, i * P : (i + 1) * P, :],
+                in0=w_flat[i][:].rearrange("p (g t) r -> p g r t", t=PACK),
+                scalar1=1.0,
+                scalar2=0.0,
+                op0=ALU.mult,
+                op1=ALU.add,
+            )
+
         def quantise_w(g):
             nc.vector.quantize_mx(
                 out=w_codes[:, g * C_OUT : (g + 1) * C_OUT].bitcast(FP8X4),
@@ -227,7 +245,7 @@ def tile_attention2_pa_kernel(tc, q, k, v, w_proj, out):
 
         def maximum_step(u, bank):
             if bank == 1:
-                running[u] = double.tile([P, HEADS_PER_BANK, CHUNK, PACK], F32, name="run")
+                running[u] = fourfold.tile([P, HEADS_PER_BANK, CHUNK, PACK], F32, name="run")
             so_far = seeds[u] if bank == 1 else running[u]
             for i in range(HEADS_PER_BANK):
                 nc.vector.tensor_tensor(
@@ -299,11 +317,16 @@ def tile_attention2_pa_kernel(tc, q, k, v, w_proj, out):
                 cols = slice(i * P, (i + 1) * P)
                 nc.tensor.transpose(recips_ps[m][:, cols], recips_t[m][:, cols], identity_f32[:])
 
-        def copy_reciprocals(m):
-            both = double.tile([P, TILE_COLS], F32, name="recip_both")
-            nc.vector.tensor_copy(out=both[:], in_=recips_ps[m][:])
-            recips[2 * m] = both[:, :UNIT_COLS]
-            recips[2 * m + 1] = both[:, UNIT_COLS:]
+        def copy_reciprocals(m, copy, place=None):
+            if place is None:
+                both = double.tile([P, TILE_COLS], F32, name="recip_both")
+                copy(out=both[:], in_=recips_ps[m][:])
+                recips[2 * m] = both[:, :UNIT_COLS]
+                recips[2 * m + 1] = both[:, UNIT_COLS:]
+            else:
+                copy(out=place[:].rearrange("p i n t -> p (i n t)"), in_=recips_ps[m][:])
+                for i in range(2):
+                    recips[2 * m + i] = place[:, i].rearrange("p n t -> p (n t)")
 
         def hand_over_reciprocals(u):
             copy = double.tile([P, UNIT_COLS], F32, name="recip_odd")
@@ -468,7 +491,7 @@ def tile_attention2_pa_kernel(tc, q, k, v, w_proj, out):
 
             if s < GPSIMD_SHIFTS and (s >= 4):
                 seed_maximum(s + 1)
-            kq_on_vector = s in (2, 3, 4)
+            kq_on_vector = s in (3, 4)
             if not kq_on_vector:
                 for kind, b, x in turn_kq.get(s - 1, ()):
                     (copy_k if kind == "k" else copy_q)(b, x, nc.scalar.copy)
@@ -488,7 +511,10 @@ def tile_attention2_pa_kernel(tc, q, k, v, w_proj, out):
                     transpose_w(i)
                     copy_w(i, nc.scalar.copy)
             for i in turn_w.get(s - 1, ()):
-                copy_w(i, nc.scalar.copy)
+                if i < 4:
+                    copy_w(i, nc.scalar.copy)
+                else:
+                    copy_w_flat(i)
             if m_y is not None:
                 store(m_y, 1, nc.scalar.copy)
             for m in logs_now:
@@ -506,7 +532,7 @@ def tile_attention2_pa_kernel(tc, q, k, v, w_proj, out):
             if s == 7:
                 for g in range(PASSES):
                     quantise_w(g)
-            if s == 5:
+            if s == 6:
                 quantise_v(1)
             if m_o is not None:
                 quantise_o(m_o)
@@ -514,7 +540,10 @@ def tile_attention2_pa_kernel(tc, q, k, v, w_proj, out):
                 quantise_attn(m_attn)
             maximum_end(s)
             if m_turn is not None:
-                copy_reciprocals(m_turn)
+                if s in (10,):
+                    copy_reciprocals(m_turn, nc.scalar.copy, running[s])
+                else:
+                    copy_reciprocals(m_turn, nc.vector.tensor_copy)
             elif unit(s - 6):
                 hand_over_reciprocals(s - 6)
             for bank in range(SCORE_BANKS):
@@ -537,14 +566,18 @@ def tile_attention2_pa_kernel(tc, q, k, v, w_proj, out):
                 project(m_o)
             if m_av is not None:
                 attention_times_v(m_av)
-            if unit(s - 1):
-                sum_over_heads(s - 1)
+            for u in range(UNITS):
+                if s == u + (2 if u in (2, 3, 4, 6, 7, 8) else 1):
+                    sum_over_heads(u)
 
-            if s < 2 * FRAMES:
-                for h in range(s % 2 * half, s % 2 * half + half):
-                    group_v_head(s // 2, h)
+            if s in (0, 1, 3, 4):
+                b_v, first = divmod(half * (0, 1, 3, 4).index(s), HEADS)
+                for h in range(first, first + half):
+                    group_v_head(b_v, h)
             if s == 1:
                 load_v(1)
+            for i in {2: (4, 5), 5: (6, 7)}.get(s, ()):
+                group_w(i)
             if unit(s - 6):
                 normalise(s - 6, nc.gpsimd, 0, HEADS, recips[s - 6])
 
@@ -562,7 +595,7 @@ def tile_attention2_pa_kernel(tc, q, k, v, w_proj, out):
         reciprocal_of_sums(7)
         normalise(11, nc.vector, 0, 8, factors(11))
         quantise_attn(4)
-        copy_reciprocals(5)
+        copy_reciprocals(5, vec)
         normalise(10, nc.gpsimd, 0, 8, recips[10])
         normalise(12, nc.vector, 0, 8, factors(12))
         normalise(13, nc.vector, 0, 8, factors(13))
@@ -580,7 +613,7 @@ def tile_attention2_pa_kernel(tc, q, k, v, w_proj, out):
         attention_times_v(5)
         quantise_o(4)
         project(4)
-        copy_reciprocals(7)
+        copy_reciprocals(7, vec)
         normalise(14, nc.gpsimd, 4, 8, recips[14])
         normalise(14, nc.vector, 0, 4, factors(14))
         normalise(15, nc.vector, 4, 8, factors(15))

@@ -454,12 +454,12 @@ def tile_attention2_pa_kernel(tc, q, k, v, w_proj, out):
         transpose_k(0, 1)
         copy_k(0, 1, nc.vector.tensor_copy)
         transpose_k(0, 2)
-        copy_k(0, 2, nc.scalar.copy)
         score_matmuls(0, 0)
-        transpose_k(0, 3)
-        copy_k(0, 3, nc.vector.tensor_copy)
         seed_maximum(0)
+        copy_k(0, 2, nc.vector.tensor_copy)
         score_matmuls(0, 1)
+        transpose_k(0, 3)
+        copy_k(0, 3, nc.scalar.copy)
         score_matmuls(0, 2)
         score_matmuls(0, 3)
         transpose_q(0, 1)

from contextlib import ExitStack

import concourse.mybir as mybir
from concourse.masks import make_identity

F32 = mybir.dt.float32
BF16 = mybir.dt.bfloat16
U32 = mybir.dt.uint32
U8 = mybir.dt.uint8
FP8X4 = mybir.dt.float8_e4m3fn_x4
ALU = mybir.AluOpType
ACT = mybir.ActivationFunctionType

P = 128
PACK = 4
FRAMES = 2
HEADS = 8
TOKENS = 512
HEAD_DIM = 128
CHANNELS = HEADS * HEAD_DIM
C_OUT = 1024
PASSES = CHANNELS // (P * PACK)
BANK = 512

CHUNK = 64
UNIT_COLS = CHUNK * PACK
UNITS_PER_FRAME = TOKENS // CHUNK
UNITS = FRAMES * UNITS_PER_FRAME
HEADS_PER_BANK = BANK // UNIT_COLS
SCORE_BANKS = HEADS // HEADS_PER_BANK
TILE_Q = 128
TILE_COLS = TILE_Q * PACK
TILES_PER_FRAME = TOKENS // TILE_Q

FLOPS = 2 * FRAMES * HEADS * TOKENS * TOKENS * HEAD_DIM * 2 + 2 * FRAMES * TOKENS * CHANNELS * C_OUT


SUM_BLOCKS = UNIT_COLS // P
LAST_TILE = UNITS // 2 - 1
TAIL_RECIP = 5
W_ON_SUMS = (0, 1, 3, 6)
GPSIMD_SHIFTS = 6
LOGS = {3: (0,), 7: (1, 2), 11: (3, 4), 13: (5,), 15: (6,)}
TAIL_TILE = 3


def tile_attention2_pa_kernel(tc, q, k, v, w_proj, out):
    nc = tc.nc
    with ExitStack() as stack:
        stack.enter_context(tc.manual_schedule())
        const = stack.enter_context(tc.tile_pool(name="const", bufs=1))
        raw = stack.enter_context(tc.tile_pool(name="raw", bufs=1))
        raw2 = stack.enter_context(tc.tile_pool(name="raw2", bufs=2))
        keep = stack.enter_context(tc.tile_pool(name="keep", bufs=1))
        single = stack.enter_context(tc.tile_pool(name="single", bufs=1))
        double = stack.enter_context(tc.tile_pool(name="double", bufs=2))
        triple = stack.enter_context(tc.tile_pool(name="triple", bufs=3))
        fourfold = stack.enter_context(tc.tile_pool(name="fourfold", bufs=4))
        fourfold = stack.enter_context(tc.tile_pool(name="fourfold", bufs=4))
        deep = stack.enter_context(tc.tile_pool(name="deep", bufs=7))
        score_psum = stack.enter_context(tc.psum_pool(name="score_psum", bufs=1))
        sum_psum = stack.enter_context(tc.psum_pool(name="sum_psum", bufs=2))
        aux_psum = stack.enter_context(tc.psum_pool(name="aux_psum", bufs=2))

        def rows_by_four(src):
            return src.rearrange("h (p x) d -> p h x d", x=PACK)

        k_raw = {}
        q_raw = {}
        v_raw = {}

        def load_k(b, pieces):
            k_raw[b] = raw.tile([P, HEADS, PACK, HEAD_DIM], BF16, name="k_raw")
            width = HEADS // pieces
            for h0 in range(0, HEADS, width):
                nc.sync.dma_start(
                    out=k_raw[b][:, h0 : h0 + width].rearrange("p h x d -> p h (x d)"),
                    in_=k[b, h0 : h0 + width].rearrange("h (p x) d -> p h (x d)", x=PACK),
                )

        def load_q(b, j0, j1):
            if j0 == 0:
                q_raw[b] = raw2.tile([P, HEADS, PACK, HEAD_DIM], BF16, name="q_raw")
            nc.sync.dma_start(
                out=q_raw[b][:, :, j0:j1, :].rearrange("p h x d -> p h (x d)"),
                in_=q[b].rearrange("h (p x) d -> p h (x d)", x=PACK)[:, :, j0 * HEAD_DIM : j1 * HEAD_DIM],
            )

        def load_v(b):
            v_raw[b] = raw.tile([P, HEADS, PACK, HEAD_DIM], BF16, name="v_raw")
            nc.sync.dma_start(
                out=v_raw[b][:].rearrange("p h t d -> p h (t d)"),
                in_=v[b].rearrange("h (p t) d -> p h (t d)", t=PACK),
            )

        w_raw = []

        def load_w(i0):
            w_half = double.tile([P, 4, CHANNELS], BF16, tag="w_attn", name="w_half", align_bytes=64)
            nc.sync.dma_start(out=w_half[:], in_=w_proj.rearrange("(i p) c -> p i c", p=P)[:, i0 : i0 + 4, :])
            w_raw.append(w_half)

        load_q(0, 0, 1)
        load_k(0, 4)
        load_q(0, 1, PACK)
        load_w(0)
        load_v(0)
        load_w(4)

        identity_f32 = const.tile([P, P], F32)
        make_identity(nc, identity_f32[:])
        identity = const.tile([P, P], BF16)
        make_identity(nc, identity[:])

        kT = {}
        qT = {}
        v_grouped = {}
        v_codes = {}
        v_scales = {}
        for b in range(FRAMES):
            kT[b] = keep.tile([P, HEADS, PACK, P], BF16, name="kT%d" % b)
            qT[b] = keep.tile([P, PACK, HEADS, P], BF16, name="qT%d" % b)
            v_codes[b] = keep.tile([P, HEADS * HEAD_DIM], U32, name="v_codes%d" % b, align_bytes=64)
            v_scales[b] = keep.tile([P, HEADS * HEAD_DIM], U8, name="v_scales%d" % b, align_bytes=64)
        w_grouped = single.tile([P, PASSES, C_OUT, PACK], BF16, tag="w_y", name="w_grouped", align_bytes=64)
        w_codes = keep.tile([P, PASSES * C_OUT], U32, align_bytes=64)
        w_scales = keep.tile([P, PASSES * C_OUT], U8, align_bytes=64)

        turned = {}

        def transpose_k(b, pair):
            if b == 0 and pair in (1, 2):
                ps = sum_psum.tile([P, 2, PACK, P], BF16, tag="sum", name="k_ps")
            else:
                ps = aux_psum.tile([P, 2, PACK, P], BF16, tag="aux", name="k_ps")
            for i in range(2):
                for t in range(PACK):
                    nc.tensor.transpose(ps[:, i, t, :], k_raw[b][:, 2 * pair + i, t, :], identity[:])
            turned["k", b, pair] = ps

        def copy_k(b, pair, copy):
            copy(out=kT[b][:, 2 * pair : 2 * pair + 2, :, :], in_=turned["k", b, pair][:])

        def transpose_q(b, j):
            ps = aux_psum.tile([P, HEADS, P], BF16, tag="aux", name="q_ps")
            for h in range(HEADS):
                nc.tensor.transpose(ps[:, h, :], q_raw[b][:, h, j, :], identity[:])
            turned["q", b, j] = ps

        def copy_q(b, j, copy):
            copy(out=qT[b][:, j, :, :], in_=turned["q", b, j][:])

        def group_v_head(b, h):
            if h == 0:
                v_grouped[b] = single.tile([P, HEADS, HEAD_DIM, PACK], BF16, name="v_grouped", align_bytes=64)
            nc.gpsimd.tensor_scalar(
                out=v_grouped[b][:, h, :, :],
                in0=v_raw[b][:, h, :, :].rearrange("p t d -> p d t"),
                scalar1=1.0,
                scalar2=0.0,
                op0=ALU.mult,
                op1=ALU.add,
            )

        def quantise_v(b):
            nc.vector.quantize_mx(
                out=v_codes[b][:].bitcast(FP8X4),
                scales=v_scales[b][:],
                in_=v_grouped[b][:].rearrange("p h d t -> p (h d t)"),
            )

        def transpose_w(i):
            if i not in W_ON_SUMS:
                ps = aux_psum.tile([P, PASSES * PACK, P], BF16, tag="aux", name="w_ps")
            else:
                ps = sum_psum.tile([P, PASSES * PACK, P], BF16, tag="sum", name="w_ps")
            for c in range(PASSES * PACK):
                nc.tensor.transpose(ps[:, c, :], w_raw[i // 4][:, i % 4, c * P : (c + 1) * P], identity[:])
            turned["w", i] = ps

        def copy_w(i, copy):
            copy(
                out=w_grouped[:, :, i * P : (i + 1) * P, :],
                in_=turned["w", i][:].rearrange("p (g t) r -> p g r t", t=PACK),
            )

        w_flat = {}

        def copy_w_flat(i):
            w_flat[i] = fourfold.tile([P, PASSES * PACK, P], BF16, name="w_flat")
            nc.scalar.copy(out=w_flat[i][:], in_=turned["w", i][:])

        def group_w(i):
            nc.gpsimd.tensor_scalar(
                out=w_grouped[:, :, i * P : (i + 1) * P, :],
                in0=w_flat[i][:].rearrange("p (g t) r -> p g r t", t=PACK),
                scalar1=1.0,
                scalar2=0.0,
                op0=ALU.mult,
                op1=ALU.add,
            )

        def quantise_w(g):
            nc.vector.quantize_mx(
                out=w_codes[:, g * C_OUT : (g + 1) * C_OUT].bitcast(FP8X4),
                scales=w_scales[:, g * C_OUT : (g + 1) * C_OUT],
                in_=w_grouped[:, g, :, :].rearrange("p r t -> p (r t)"),
            )

        scores = {}
        seeds = {}
        running = {}
        tops = {}
        expd = {}
        totals = {}

        def frame_of(u):
            return u // UNITS_PER_FRAME

        def score_matmuls(u, bank):
            b = frame_of(u)
            first = (u % UNITS_PER_FRAME) * CHUNK
            j, col = first // P, first % P
            if bank == 0:
                scores[u] = []
            s_ps = score_psum.tile([P, HEADS_PER_BANK, PACK, CHUNK], F32, name="s_ps%d" % bank)
            for i in range(HEADS_PER_BANK):
                h = bank * HEADS_PER_BANK + i
                for t in range(PACK):
                    nc.tensor.matmul(
                        out=s_ps[:, i, t, :],
                        lhsT=kT[b][:, h, t, :],
                        rhs=qT[b][:, j, h, col : col + CHUNK],
                        start=True,
                        stop=True,
                    )
            scores[u].append(s_ps)

        def bank_view(s_ps):
            return s_ps[:].rearrange("p i t n -> p i n t")

        def seed_maximum(u):
            seeds[u] = double.tile([P, HEADS_PER_BANK, CHUNK, PACK], F32, name="seed")
            nc.scalar.copy(out=seeds[u][:], in_=bank_view(scores[u][0]))

        def maximum_step(u, bank):
            if bank == 1:
                running[u] = fourfold.tile([P, HEADS_PER_BANK, CHUNK, PACK], F32, name="run")
            so_far = seeds[u] if bank == 1 else running[u]
            for i in range(HEADS_PER_BANK):
                nc.vector.tensor_tensor(
                    out=running[u][:, i],
                    in0=scores[u][bank][:, i].rearrange("p t n -> p n t"),
                    in1=so_far[:, i],
                    op=ALU.max,
                )

        def maximum_end(u):
            tops[u] = double.tile([P, CHUNK, PACK], F32, name="top")
            nc.vector.tensor_tensor(out=tops[u][:], in0=running[u][:, 0], in1=running[u][:, 1], op=ALU.max)

        def shift_bank(u, bank):
            if bank == 0:
                expd[u] = deep.tile([P, HEADS, UNIT_COLS], F32, name="e")
            h0 = bank * HEADS_PER_BANK
            on_gpsimd = bank == 0 and u < GPSIMD_SHIFTS
            engine = nc.gpsimd if on_gpsimd else nc.vector
            engine.tensor_tensor(
                out=expd[u][:, h0 : h0 + HEADS_PER_BANK, :].rearrange("p i (n t) -> p i n t", t=PACK),
                in0=seeds[u][:] if on_gpsimd else bank_view(scores[u][bank]),
                in1=tops[u][:].unsqueeze(1).to_broadcast([P, HEADS_PER_BANK, CHUNK, PACK]),
                op=ALU.subtract,
            )

        def exponentials(u):
            nc.scalar.activation(out=expd[u][:], in_=expd[u][:], func=ACT.Exp, scale=HEAD_DIM**-0.5)

        def sum_over_heads(u):
            m, half = u // 2, u % 2
            if half == 0:
                totals[m] = sum_psum.tile([P, 2 * SUM_BLOCKS, P], F32, tag="sum", name="total")
            for i in range(SUM_BLOCKS):
                for h in range(HEADS):
                    nc.tensor.matmul(
                        out=totals[m][:, half * SUM_BLOCKS + i, :],
                        lhsT=expd[u][:, h, i * P : (i + 1) * P],
                        rhs=identity_f32[:],
                        start=(h == 0),
                        stop=(h == HEADS - 1),
                        is_transpose=True,
                    )

        recips_t = {}
        recips_ps = {}
        recips = {}
        attn = {}
        a_words = {}
        o_banks = {}
        o_grouped = {}
        o_words = {}
        y_banks = {}
        y_slots = {}

        def log_of_sums(m):
            recips_t[m] = double.tile([P, TILE_COLS], F32, name="recip_t")
            nc.scalar.activation(out=recips_t[m][:], in_=totals[m][:].rearrange("c i p -> c (i p)"), func=ACT.Ln)

        def reciprocal_of_sums(m):
            nc.scalar.activation(out=recips_t[m][:], in_=recips_t[m][:], func=ACT.Exp, scale=-1.0)

        def turn_reciprocals(m):
            if m < TAIL_RECIP:
                recips_ps[m] = aux_psum.tile([P, TILE_COLS], F32, tag="aux", name="recip_ps")
            else:
                recips_ps[m] = score_psum.tile([P, TILE_COLS], F32, name="s_ps%d" % (m % 2))
            for i in range(TILE_COLS // P):
                cols = slice(i * P, (i + 1) * P)
                nc.tensor.transpose(recips_ps[m][:, cols], recips_t[m][:, cols], identity_f32[:])

        def copy_reciprocals(m, copy, place=None):
            if place is None:
                both = double.tile([P, TILE_COLS], F32, name="recip_both")
                copy(out=both[:], in_=recips_ps[m][:])
                recips[2 * m] = both[:, :UNIT_COLS]
                recips[2 * m + 1] = both[:, UNIT_COLS:]
            else:
                copy(out=place[:].rearrange("p i n t -> p (i n t)"), in_=recips_ps[m][:])
                for i in range(2):
                    recips[2 * m + i] = place[:, i].rearrange("p n t -> p (n t)")

        def hand_over_reciprocals(u):
            copy = double.tile([P, UNIT_COLS], F32, name="recip_odd")
            nc.vector.tensor_copy(out=copy[:], in_=recips[u])
            recips[u] = copy[:]

        def normalise(u, engine, h0, h1, factors):
            m, half = u // 2, u % 2
            if m not in attn:
                attn[m] = double.tile([P, HEADS, TILE_COLS], BF16, tag="w_attn", name="attn", align_bytes=64)
            engine.tensor_tensor(
                out=attn[m][:, h0:h1, half * UNIT_COLS : (half + 1) * UNIT_COLS],
                in0=expd[u][:, h0:h1, :],
                in1=factors.unsqueeze(1).to_broadcast([P, h1 - h0, UNIT_COLS]),
                op=ALU.mult,
            )

        def quantise_attn(m, g0=0, g1=PASSES):
            if g0 == 0:
                a_codes = triple.tile([P, HEADS * TILE_Q], U32, align_bytes=64)
                a_scales = triple.tile([P, HEADS * TILE_Q], U8, align_bytes=64)
                a_words[m] = (a_codes, a_scales)
            a_codes, a_scales = a_words[m]
            cols = slice(g0 * PACK * TILE_Q, g1 * PACK * TILE_Q)
            nc.vector.quantize_mx(
                out=a_codes[:, cols].bitcast(FP8X4),
                scales=a_scales[:, cols],
                in_=attn[m][:, g0 * PACK : g1 * PACK, :].rearrange("p h c -> p (h c)"),
            )

        def attention_times_v(m, groups=range(PASSES)):
            b = m // TILES_PER_FRAME
            a_codes, a_scales = a_words[m]
            if m not in o_banks:
                o_banks[m] = []
            for g in groups:
                o_ps = aux_psum.tile([P, PACK, TILE_Q], F32, tag="aux", name="o_ps")
                for t in range(PACK):
                    h = g * PACK + t
                    cols = slice(h * TILE_Q, (h + 1) * TILE_Q)
                    nc.tensor.matmul_mx(
                        out=o_ps[:, t, :],
                        lhsT=v_codes[b][:, cols].bitcast(FP8X4),
                        lhsT_scale=v_scales[b][:, cols],
                        rhs=a_codes[:, cols].bitcast(FP8X4),
                        rhs_scale=a_scales[:, cols],
                        start=True,
                        stop=True,
                    )
                o_banks[m].append(o_ps)

        def round_o(m, g, copy):
            if g == 0:
                o_grouped[m] = triple.tile([P, PASSES, TILE_Q, PACK], BF16, name="o_grouped", align_bytes=64)
            copy(out=o_grouped[m][:, g, :, :], in_=o_banks[m][g][:].rearrange("p t n -> p n t"))

        def quantise_o(m, g0=0, g1=PASSES):
            if g0 == 0:
                o_codes = triple.tile([P, PASSES * TILE_Q], U32, align_bytes=64)
                o_scales = triple.tile([P, PASSES * TILE_Q], U8, align_bytes=64)
                o_words[m] = (o_codes, o_scales)
            o_codes, o_scales = o_words[m]
            cols = slice(g0 * TILE_Q, g1 * TILE_Q)
            nc.vector.quantize_mx(
                out=o_codes[:, cols].bitcast(FP8X4),
                scales=o_scales[:, cols],
                in_=o_grouped[m][:, g0:g1].rearrange("p g n t -> p (g n t)"),
            )

        def project(m):
            open_projection(m)
            for i in range(C_OUT // BANK):
                for g in range(PASSES):
                    project_pass(m, i, g)

        def open_projection(m):
            y_banks[m] = []
            for i in range(C_OUT // BANK):
                if m < TAIL_TILE:
                    y_ps = aux_psum.tile([P, BANK], F32, tag="aux", name="y_ps")
                elif m in (4, 6):
                    y_ps = sum_psum.tile([P, BANK], F32, tag="sum", name="y_ps")
                else:
                    y_ps = score_psum.tile([P, BANK], F32, name="s_ps%d" % (i if m == LAST_TILE else 2 + i))
                y_banks[m].append(y_ps)

        def project_pass(m, i, g):
            o_codes, o_scales = o_words[m]
            o_cols = slice(g * TILE_Q, (g + 1) * TILE_Q)
            w_cols = slice(g * C_OUT + i * BANK, g * C_OUT + (i + 1) * BANK)
            nc.tensor.matmul_mx(
                out=y_banks[m][i][:],
                lhsT=o_codes[:, o_cols].bitcast(FP8X4),
                lhsT_scale=o_scales[:, o_cols],
                rhs=w_codes[:, w_cols].bitcast(FP8X4),
                rhs_scale=w_scales[:, w_cols],
                start=(g == 0),
                stop=(g == PASSES - 1),
            )

        def store(m, i, copy):
            b, j = divmod(m, TILES_PER_FRAME)
            if m == 0 and not y_slots:
                y_slots[0] = single.tile([P, 2 * PACK, BANK], F32, tag="w_y", name="y_slots", align_bytes=64)
            y = y_slots[0][:, (2 * m + i) % (2 * PACK), :]
            copy(out=y, in_=y_banks[m][i][:])
            nc.sync.dma_start(
                out=out[b].rearrange("(p j) c -> p j c", j=PACK)[:, j, i * BANK : (i + 1) * BANK], in_=y
            )

        def unit(u):
            return 0 <= u < UNITS

        def tile_at(s, first):
            m, rest = divmod(s - first, 2)
            return m if rest == 0 and 0 <= m <= LAST_TILE else None

        idle_ps = score_psum.tile([P, P], F32, name="s_ps3")
        for i in range(6):
            nc.tensor.matmul(out=idle_ps[:], lhsT=identity_f32[:], rhs=identity_f32[:], start=True, stop=True)
        transpose_q(0, 0)
        copy_q(0, 0, nc.vector.tensor_copy)
        transpose_k(0, 0)
        copy_k(0, 0, nc.scalar.copy)
        transpose_k(0, 1)
        copy_k(0, 1, nc.vector.tensor_copy)
        transpose_k(0, 2)
        score_matmuls(0, 0)
        seed_maximum(0)
        copy_k(0, 2, nc.vector.tensor_copy)
        score_matmuls(0, 1)
        transpose_k(0, 3)
        copy_k(0, 3, nc.scalar.copy)
        score_matmuls(0, 2)
        score_matmuls(0, 3)
        transpose_q(0, 1)
        copy_q(0, 1, nc.scalar.copy)
        score_matmuls(1, 0)
        load_k(1, 1)
        load_q(1, 0, PACK)

        turn_kq = {
            1: (("q", 0, 2),),
            2: (("k", 1, 0),),
            3: (("q", 0, 3),),
            4: (("k", 1, 1), ("k", 1, 2)),
            5: (("k", 1, 3), ("q", 1, 0)),
            6: (("q", 1, 1),),
            8: (("q", 1, 2), ("q", 1, 3)),
        }
        turn_w = {0: (3, 4), 1: (5,), 2: (6,), 3: (7,)}

        half = HEADS // 2
        for s in range(UNITS):
            m_turn = tile_at(s, 6)
            m_attn = tile_at(s, 8)
            m_av = tile_at(s, 9)
            m_o = tile_at(s, 10)
            m_y = tile_at(s, 11)
            logs_now = LOGS.get(s, ())
            exps_now = LOGS.get(s - 1, ())

            if s < GPSIMD_SHIFTS and (s >= 4):
                seed_maximum(s + 1)
            kq_on_vector = s in (3, 4)
            if not kq_on_vector:
                for kind, b, x in turn_kq.get(s - 1, ()):
                    (copy_k if kind == "k" else copy_q)(b, x, nc.scalar.copy)
            if m_o is not None:
                for g in range(PASSES):
                    round_o(m_o, g, nc.scalar.copy)
            for m in exps_now[:1]:
                reciprocal_of_sums(m)
            if m_turn is not None:
                turn_reciprocals(m_turn)
            if unit(s - 1):
                exponentials(s - 1)
            if s < GPSIMD_SHIFTS and not (s >= 4):
                seed_maximum(s + 1)
            if s == 0:
                for i in range(3):
                    transpose_w(i)
                    copy_w(i, nc.scalar.copy)
            for i in turn_w.get(s - 1, ()):
                if i < 4:
                    copy_w(i, nc.scalar.copy)
                else:
                    copy_w_flat(i)
            if m_y is not None:
                store(m_y, 1, nc.scalar.copy)
            for m in logs_now:
                log_of_sums(m)

            for bank in range(1, SCORE_BANKS):
                maximum_step(s, bank)
            if kq_on_vector:
                for kind, b, x in turn_kq.get(s - 1, ()):
                    (copy_k if kind == "k" else copy_q)(b, x, nc.vector.tensor_copy)
            if m_y is not None:
                store(m_y, 0, nc.vector.tensor_copy)
            if s == 2:
                quantise_v(0)
            if s == 7:
                for g in range(PASSES):
                    quantise_w(g)
            if s == 6:
                quantise_v(1)
            if m_o is not None:
                quantise_o(m_o)
            if m_attn is not None:
                quantise_attn(m_attn)
            maximum_end(s)
            if m_turn is not None:
                if s in (10,):
                    copy_reciprocals(m_turn, nc.scalar.copy, running[s])
                else:
                    copy_reciprocals(m_turn, nc.vector.tensor_copy)
            elif unit(s - 6):
                hand_over_reciprocals(s - 6)
            for bank in range(SCORE_BANKS):
                shift_bank(s, bank)
                if unit(s + 1) and (bank or s >= GPSIMD_SHIFTS):
                    score_matmuls(s + 1, bank)
                    if bank == 0:
                        seed_maximum(s + 1)
            if s + 1 < GPSIMD_SHIFTS:
                score_matmuls(s + 2, 0)

            for m in exps_now[1:]:
                reciprocal_of_sums(m)

            for kind, b, x in turn_kq.get(s, ()):
                (transpose_k if kind == "k" else transpose_q)(b, x)
            for i in turn_w.get(s, ()):
                transpose_w(i)
            if m_o is not None:
                project(m_o)
            if m_av is not None:
                attention_times_v(m_av)
            for u in range(UNITS):
                if s == u + (2 if u in (2, 3, 4, 6, 7, 8) else 1):
                    sum_over_heads(u)

            if s in (0, 1, 3, 4):
                b_v, first = divmod(half * (0, 1, 3, 4).index(s), HEADS)
                for h in range(first, first + half):
                    group_v_head(b_v, h)
            if s == 1:
                load_v(1)
            for i in {2: (4, 5), 5: (6, 7)}.get(s, ()):
                group_w(i)
            if unit(s - 6):
                normalise(s - 6, nc.gpsimd, 0, HEADS, recips[s - 6])

        vec, sca = nc.vector.tensor_copy, nc.scalar.copy

        def factors(u):
            return recips_ps[u // 2][:, u % 2 * UNIT_COLS : (u % 2 + 1) * UNIT_COLS]

        turn_reciprocals(5)
        reciprocal_of_sums(6)
        exponentials(15)
        turn_reciprocals(6)
        sum_over_heads(15)
        log_of_sums(7)
        reciprocal_of_sums(7)
        normalise(11, nc.vector, 0, 8, factors(11))
        quantise_attn(4)
        copy_reciprocals(5, vec)
        normalise(10, nc.gpsimd, 0, 8, recips[10])
        normalise(12, nc.vector, 0, 8, factors(12))
        normalise(13, nc.vector, 0, 8, factors(13))
        turn_reciprocals(7)
        round_o(3, 0, sca)
        round_o(3, 1, sca)
        attention_times_v(4)
        quantise_attn(5)
        quantise_attn(6)
        quantise_o(3)
        project(3)
        normalise(15, nc.vector, 0, 4, factors(15))
        round_o(4, 0, sca)
        round_o(4, 1, sca)
        attention_times_v(5)
        quantise_o(4)
        project(4)
        copy_reciprocals(7, vec)
        normalise(14, nc.gpsimd, 4, 8, recips[14])
        normalise(14, nc.vector, 0, 4, factors(14))
        normalise(15, nc.vector, 4, 8, factors(15))
        store(3, 0, sca)
        store(3, 1, sca)
        round_o(5, 0, sca)
        round_o(5, 1, sca)
        attention_times_v(6)
        store(4, 0, sca)
        store(4, 1, sca)
        round_o(6, 0, sca)
        round_o(6, 1, sca)
        quantise_o(5)
        project(5)
        quantise_attn(7, 0, 1)
        attention_times_v(7, (0,))
        quantise_attn(7, 1, 2)
        quantise_o(6)
        attention_times_v(7, (1,))
        project(6)
        round_o(7, 0, sca)
        round_o(7, 1, vec)
        store(5, 0, sca)
        store(5, 1, vec)
        quantise_o(7, 0, 1)
        open_projection(7)
        for i in range(C_OUT // BANK):
            project_pass(7, i, 0)
        quantise_o(7, 1, 2)
        for i in range(C_OUT // BANK):
            project_pass(7, i, 1)
        store(6, 0, sca)
        store(6, 1, vec)
        store(7, 0, sca)
        store(7, 1, vec)
